import numpy as np
import ml_dtypes


def mxq(x, axis, fmt="e4m3"):
    dtype, down = {"e4m3": (ml_dtypes.float8_e4m3fn, 7), "e5m2": (ml_dtypes.float8_e5m2, 14)}[fmt]
    v = np.moveaxis(np.asarray(x, np.float32).astype(ml_dtypes.bfloat16).astype(np.float64), axis, -1)
    blocks = v.reshape(v.shape[:-1] + (-1, 32))
    amax = np.abs(blocks).max(-1, keepdims=True)
    byte = np.maximum(np.where(amax > 0, np.frexp(amax)[1] - 1 + 127, 0) - down, 1)
    scale = np.exp2(byte - 127.0)
    codes = (blocks / scale).astype(np.float32).astype(dtype).astype(np.float64)
    return np.moveaxis((codes * scale).reshape(v.shape), -1, axis)


BF16 = ml_dtypes.bfloat16


def bf(x):
    return np.asarray(x, np.float32).astype(BF16)


def f64(x):
    return np.asarray(x).astype(np.float64)


N, K, C, M, R, L = 128, 16384, 16, 8, 2, 8

LN_EPS = 1e-5


def layer_norm(x, w, b):
    mu = np.mean(x, axis=-1, keepdims=True)
    var = np.var(x, axis=-1, keepdims=True)
    return (x - mu) / np.sqrt(var + LN_EPS) * w + b


def l2_normalize(x, eps=1e-12):
    n = np.sqrt(np.sum(x * x, axis=-1, keepdims=True))
    return x / np.maximum(n, eps)


def clustered(rows, centres, a, b):
    return a * centres[np.random.randint(L, size=rows)] + b * np.random.standard_normal((rows, K))


def setup_inputs():
    cx = np.random.standard_normal((L, K))
    cv = np.random.standard_normal((L, K))
    x = clustered(N, cx, 0.7, 0.4) + 0.5 * np.random.standard_normal((N, 1))
    x_var = -1.0 + clustered(N, cv, 0.6, 0.5)
    prototypes = (clustered(C * M, cx, 0.7, 0.4) + 0.5 * np.random.standard_normal((C * M, 1))).reshape(C, M, K)
    proto_var = (-0.5 + clustered(C * M, cv, 0.6, 0.5)).reshape(C, M, K)
    return {"x": bf(x), "x_var": bf(x_var), "prototypes": bf(prototypes), "proto_var": bf(proto_var),
            "eps_x": bf(np.random.standard_normal((R, N, K))), "eps_p": bf(np.random.standard_normal((R, C, M, K))),
            "ln_w": bf(1.5 + 0.5 * np.random.standard_normal(K)), "ln_b": bf(0.5 * np.random.standard_normal(K))}


def reference(x, x_var, prototypes, proto_var, eps_x, eps_p, ln_w, ln_b):
    x, x_var, prototypes, proto_var = f64(x), f64(x_var), f64(prototypes), f64(proto_var)
    eps_x, eps_p, ln_w, ln_b = f64(eps_x), f64(eps_p), f64(ln_w), f64(ln_b)
    lamda = 1.0 / (K // 4)
    p_s = eps_p * np.exp(0.5 * proto_var) + prototypes
    p_s = l2_normalize(layer_norm(p_s, ln_w, ln_b))
    x_s = eps_x * np.exp(0.5 * x_var) + x
    x_s = l2_normalize(layer_norm(x_s, ln_w, ln_b))
    xv = np.exp(x_var)
    pv = np.exp(proto_var)
    xq = mxq(x_s, 2, "e4m3")
    pq = mxq(p_s, 3, "e4m3")
    sim = xq.reshape(R * N, K) @ pq.reshape(R * C * M, K).T
    sim = sim.reshape(R, N, R, C, M).transpose(0, 2, 1, 4, 3)
    sim = np.mean(sim.reshape((-1,) + sim.shape[2:]), axis=0)
    sim = np.transpose(sim, (2, 1, 0))
    cross = mxq(np.sqrt(xv), 1, "e4m3") @ mxq(np.sqrt(pv), 2, "e4m3").reshape(C * M, K).T
    cross = cross.T.reshape(C, M, N)
    w2 = (2.0 - 2.0 * sim
          + lamda * (np.sum(xv, axis=-1)
                     + np.sum(pv, axis=-1, keepdims=True)
                     - 2.0 * cross))
    return -np.transpose(w2, (2, 0, 1))

@@ -1,0 +1,251 @@
+from contextlib import ExitStack
+
+import concourse.mybir as mybir
+from concourse.masks import make_identity
+
+F32 = mybir.dt.float32
+BF16 = mybir.dt.bfloat16
+U32 = mybir.dt.uint32
+U8 = mybir.dt.uint8
+FP8X4 = mybir.dt.float8_e4m3fn_x4
+ALU = mybir.AluOpType
+ACT = mybir.ActivationFunctionType
+AXIS_X = mybir.AxisListType.X
+
+P = 128
+K = 16384
+CHUNK = 2048
+N_CHUNKS = K // CHUNK
+K_PASS = 512
+PASSES_PER_CHUNK = CHUNK // K_PASS
+WORDS_PER_CHUNK = PASSES_PER_CHUNK * P
+SAMPLES = 2
+LN_EPS = 1e-5
+LAMDA = 1.0 / (K // 4)
+CROSS_EVERY = 4
+
+FLOPS = 2 * (SAMPLES * P) * (SAMPLES * P) * K + 2 * P * P * K
+
+
+def tile_probprotoseghead_k_kernel(
+    tc, x, x_var, prototypes, proto_var, eps_x, eps_p, ln_w, ln_b, out
+):
+    nc = tc.nc
+    proto_rows = prototypes.rearrange("c m k -> (c m) k")
+    proto_var_rows = proto_var.rearrange("c m k -> (c m) k")
+
+    with ExitStack() as ctx:
+        const = ctx.enter_context(tc.tile_pool(name="const", bufs=1))
+        vpool = ctx.enter_context(tc.tile_pool(name="vpool", bufs=N_CHUNKS))
+        loads = ctx.enter_context(tc.tile_pool(name="loads", bufs=3))
+        rows = ctx.enter_context(tc.tile_pool(name="rows", bufs=2))
+        packs = ctx.enter_context(tc.tile_pool(name="packs", bufs=2))
+        small = ctx.enter_context(tc.tile_pool(name="small", bufs=2))
+        flipped = ctx.enter_context(tc.psum_pool(name="flipped", bufs=4))
+        sums = ctx.enter_context(tc.psum_pool(name="sums", bufs=1))
+
+        ident = const.tile([P, P], F32)
+        make_identity(nc, ident[:])
+        ones = const.tile([P, P], F32)
+        nc.vector.memset(ones[:], 1.0)
+        neg_half = const.tile([P, 1], F32)
+        nc.vector.memset(neg_half[:], -0.5)
+
+        w_all = const.tile([P, K], BF16)
+        b_all = const.tile([P, K], BF16)
+
+        x_codes0 = const.tile([P, N_CHUNKS * WORDS_PER_CHUNK], U32, align_bytes=64)
+        x_codes1 = const.tile([P, N_CHUNKS * WORDS_PER_CHUNK], U32, align_bytes=64)
+        x_scales0 = const.tile([P, N_CHUNKS * WORDS_PER_CHUNK], U8, align_bytes=64)
+        x_scales1 = const.tile([P, N_CHUNKS * WORDS_PER_CHUNK], U8, align_bytes=64)
+        x_codes = [x_codes0, x_codes1]
+        x_scales = [x_scales0, x_scales1]
+
+        sim_sum = sums.tile([P, P], F32)
+        cross_sum = sums.tile([P, P], F32)
+        xv_parts = const.tile([P, N_CHUNKS], F32)
+        pv_parts = const.tile([P, N_CHUNKS], F32)
+
+        def quantise_rows(row16, codes, scales):
+            words = row16[:].bitcast(F32).rearrange(
+                "p (g q u) -> p g u q", g=PASSES_PER_CHUNK, u=2
+            )
+            grouped = packs.tile([P, CHUNK], BF16, align_bytes=64)
+            grouped_words = grouped[:].bitcast(F32).rearrange(
+                "p (h g n u) -> p h g n u", h=PASSES_PER_CHUNK // 2, g=2, u=2
+            )
+            for h in range(PASSES_PER_CHUNK // 2):
+                bank = flipped.tile([P, 2, 2, P], F32)
+                for g in range(2):
+                    for u in range(2):
+                        nc.tensor.transpose(bank[:, g, u, :], words[:, 2 * h + g, u, :], ident[:])
+                nc.scalar.copy(
+                    out=grouped_words[:, h], in_=bank[:].rearrange("p g u n -> p g n u")
+                )
+            nc.vector.quantize_mx(out=codes.bitcast(FP8X4), scales=scales, in_=grouped[:])
+
+        def cross_chunk(j):
+            cols = slice(j * CHUNK, (j + 1) * CHUNK)
+            operands = []
+            for logvar_rows, parts in ((x_var, xv_parts), (proto_var_rows, pv_parts)):
+                logvar = loads.tile([P, CHUNK], BF16, tag="logvar")
+                nc.sync.dma_start(out=logvar[:], in_=logvar_rows[:, cols])
+                std16 = rows.tile([P, CHUNK], BF16, tag="row16")
+                nc.scalar.activation(out=std16[:], in_=logvar[:], func=ACT.Exp, scale=0.5)
+                nc.scalar.activation(
+                    out=logvar[:], in_=logvar[:], func=ACT.Exp, accum_out=parts[:, j : j + 1]
+                )
+                codes = packs.tile([P, WORDS_PER_CHUNK], U32, align_bytes=64, tag="codes")
+                scales = packs.tile([P, WORDS_PER_CHUNK], U8, align_bytes=64, tag="scales")
+                quantise_rows(std16, codes[:], scales[:])
+                operands.append((codes, scales))
+            (xc, xs), (pc, ps) = operands
+            for g in range(PASSES_PER_CHUNK):
+                one = slice(g * P, (g + 1) * P)
+                nc.tensor.matmul_mx(
+                    out=cross_sum[:],
+                    lhsT=xc[:, one].bitcast(FP8X4),
+                    lhsT_scale=xs[:, one],
+                    rhs=pc[:, one].bitcast(FP8X4),
+                    rhs_scale=ps[:, one],
+                    start=(j == 0 and g == 0),
+                    stop=(j == N_CHUNKS - 1 and g == PASSES_PER_CHUNK - 1),
+                )
+
+        planes = [
+            (x, x_var, eps_x[0]),
+            (x, x_var, eps_x[1]),
+            (proto_rows, proto_var_rows, eps_p[0].rearrange("c m k -> (c m) k")),
+            (proto_rows, proto_var_rows, eps_p[1].rearrange("c m k -> (c m) k")),
+        ]
+        for plane, (mean_rows, logvar_rows, noise_rows) in enumerate(planes):
+            v_chunks = []
+            v_sum = small.tile([P, N_CHUNKS], F32)
+            v_sq = small.tile([P, N_CHUNKS], F32)
+            neg_shift = small.tile([P, 1], F32)
+            for c in range(N_CHUNKS):
+                cols = slice(c * CHUNK, (c + 1) * CHUNK)
+                logvar = loads.tile([P, CHUNK], BF16, tag="logvar")
+                nc.sync.dma_start(out=logvar[:], in_=logvar_rows[:, cols])
+                noise = loads.tile([P, CHUNK], BF16)
+                nc.sync.dma_start(out=noise[:], in_=noise_rows[:, cols])
+                mean = loads.tile([P, CHUNK], BF16)
+                nc.sync.dma_start(out=mean[:], in_=mean_rows[:, cols])
+                v = vpool.tile([P, CHUNK], F32)
+                nc.scalar.activation(out=v[:], in_=logvar[:], func=ACT.Exp, scale=0.5)
+                nc.vector.tensor_mul(out=v[:], in0=noise[:], in1=v[:])
+                nc.vector.scalar_tensor_tensor(
+                    out=v[:], in0=v[:], scalar=1.0, in1=mean[:], op0=ALU.mult, op1=ALU.add,
+                    accum_out=v_sum[:, c : c + 1],
+                )
+                if c == 0:
+                    nc.vector.tensor_scalar_mul(
+                        out=neg_shift[:], in0=v_sum[:, 0:1], scalar1=-1.0 / CHUNK
+                    )
+                squares = rows.tile([P, CHUNK], BF16, tag="squares")
+                nc.scalar.activation(
+                    out=squares[:], in_=v[:], func=ACT.Square, bias=neg_shift[:],
+                    accum_out=v_sq[:, c : c + 1],
+                )
+                v_chunks.append(v)
+            if plane == 0:
+                for c in range(N_CHUNKS):
+                    cols = slice(c * CHUNK, (c + 1) * CHUNK)
+                    nc.sync.dma_start(out=w_all[:, cols], in_=ln_w[cols].partition_broadcast(P))
+                    nc.sync.dma_start(out=b_all[:, cols], in_=ln_b[cols].partition_broadcast(P))
+
+            mu = small.tile([P, 1], F32)
+            nc.vector.reduce_sum(out=mu[:], in_=v_sum[:], axis=AXIS_X)
+            nc.vector.tensor_scalar_mul(out=mu[:], in0=mu[:], scalar1=1.0 / K)
+            off = small.tile([P, 1], F32)
+            nc.vector.tensor_add(out=off[:], in0=mu[:], in1=neg_shift[:])
+            nc.vector.tensor_mul(out=off[:], in0=off[:], in1=off[:])
+            var = small.tile([P, 1], F32)
+            nc.vector.reduce_sum(out=var[:], in_=v_sq[:], axis=AXIS_X)
+            nc.vector.scalar_tensor_tensor(
+                out=var[:], in0=var[:], scalar=1.0 / K, in1=off[:], op0=ALU.mult, op1=ALU.subtract
+            )
+            nc.vector.tensor_scalar_add(out=var[:], in0=var[:], scalar1=LN_EPS)
+            rstd = small.tile([P, 1], F32)
+            nc.gpsimd.tensor_tensor(out=rstd[:], in0=var[:], in1=neg_half[:], op=ALU.pow)
+
+            u_sq = small.tile([P, N_CHUNKS], F32)
+            for c, v in enumerate(v_chunks):
+                cols = slice(c * CHUNK, (c + 1) * CHUNK)
+                nc.vector.scalar_tensor_tensor(
+                    out=v[:], in0=v[:], scalar=mu[:], in1=w_all[:, cols],
+                    op0=ALU.subtract, op1=ALU.mult,
+                )
+                nc.vector.scalar_tensor_tensor(
+                    out=v[:], in0=v[:], scalar=rstd[:], in1=b_all[:, cols],
+                    op0=ALU.mult, op1=ALU.add,
+                )
+                squares = rows.tile([P, CHUNK], BF16, tag="squares")
+                nc.scalar.activation(
+                    out=squares[:], in_=v[:], func=ACT.Square, accum_out=u_sq[:, c : c + 1]
+                )
+                if c % CROSS_EVERY == 0:
+                    cross_chunk(plane * (N_CHUNKS // CROSS_EVERY) + c // CROSS_EVERY)
+
+            norm2 = small.tile([P, 1], F32)
+            nc.vector.reduce_sum(out=norm2[:], in_=u_sq[:], axis=AXIS_X)
+            nc.vector.tensor_scalar_max(out=norm2[:], in0=norm2[:], scalar1=1e-24)
+            inv_norm = small.tile([P, 1], F32)
+            nc.gpsimd.tensor_tensor(out=inv_norm[:], in0=norm2[:], in1=neg_half[:], op=ALU.pow)
+
+            for c, v in enumerate(v_chunks):
+                chunk_words = slice(c * WORDS_PER_CHUNK, (c + 1) * WORDS_PER_CHUNK)
+                unit16 = rows.tile([P, CHUNK], BF16, tag="row16")
+                nc.vector.tensor_scalar_mul(out=unit16[:], in0=v[:], scalar1=inv_norm[:])
+                if plane < SAMPLES:
+                    quantise_rows(
+                        unit16, x_codes[plane][:, chunk_words], x_scales[plane][:, chunk_words]
+                    )
+                    continue
+                p_codes = packs.tile([P, WORDS_PER_CHUNK], U32, align_bytes=64, tag="codes")
+                p_scales = packs.tile([P, WORDS_PER_CHUNK], U8, align_bytes=64, tag="scales")
+                quantise_rows(unit16, p_codes[:], p_scales[:])
+                for g in range(PASSES_PER_CHUNK):
+                    one = slice(g * P, (g + 1) * P)
+                    x_one = slice(c * WORDS_PER_CHUNK + g * P, c * WORDS_PER_CHUNK + (g + 1) * P)
+                    for r in range(SAMPLES):
+                        nc.tensor.matmul_mx(
+                            out=sim_sum[:],
+                            lhsT=x_codes[r][:, x_one].bitcast(FP8X4),
+                            lhsT_scale=x_scales[r][:, x_one],
+                            rhs=p_codes[:, one].bitcast(FP8X4),
+                            rhs_scale=p_scales[:, one],
+                            start=(plane == SAMPLES and c == 0 and g == 0 and r == 0),
+                            stop=(
+                                plane == 2 * SAMPLES - 1
+                                and c == N_CHUNKS - 1
+                                and g == PASSES_PER_CHUNK - 1
+                                and r == SAMPLES - 1
+                            ),
+                        )
+
+        xv_term = small.tile([P, 1], F32)
+        nc.vector.reduce_sum(out=xv_term[:], in_=xv_parts[:], axis=AXIS_X)
+        nc.vector.tensor_scalar(
+            out=xv_term[:], in0=xv_term[:], scalar1=-LAMDA, scalar2=-2.0, op0=ALU.mult, op1=ALU.add
+        )
+        pv_sum = small.tile([P, 1], F32)
+        nc.vector.reduce_sum(out=pv_sum[:], in_=pv_parts[:], axis=AXIS_X)
+        pv_repeated = small.tile([P, P], F32)
+        nc.vector.tensor_scalar_mul(out=pv_repeated[:], in0=ones[:], scalar1=pv_sum[:])
+        pv_along = sums.tile([P, P], F32)
+        nc.tensor.transpose(pv_along[:], pv_repeated[:], ident[:])
+
+        result = small.tile([P, P], F32)
+        nc.vector.tensor_scalar(
+            out=result[:], in0=cross_sum[:], scalar1=2.0 * LAMDA, scalar2=xv_term[:],
+            op0=ALU.mult, op1=ALU.add,
+        )
+        nc.vector.scalar_tensor_tensor(
+            out=result[:], in0=pv_along[:], scalar=-LAMDA, in1=result[:],
+            op0=ALU.mult, op1=ALU.add,
+        )
+        nc.vector.scalar_tensor_tensor(
+            out=result[:], in0=sim_sum[:], scalar=0.5, in1=result[:], op0=ALU.mult, op1=ALU.add
+        )
+        nc.sync.dma_start(out=out.rearrange("n c m -> n (c m)"), in_=result[:])

@@ -23,6 +23,8 @@ SAMPLES = 2
 LN_EPS = 1e-5
 LAMDA = 1.0 / (K // 4)
 CROSS_EVERY = 4
+BANK_BF16 = 1024
+V_SLOTS = 14
 
 FLOPS = 2 * (SAMPLES * P) * (SAMPLES * P) * K + 2 * P * P * K
 
@@ -36,12 +38,13 @@ def tile_probprotoseghead_k_kernel(
 
     with ExitStack() as ctx:
         const = ctx.enter_context(tc.tile_pool(name="const", bufs=1))
-        vpool = ctx.enter_context(tc.tile_pool(name="vpool", bufs=N_CHUNKS))
+        vpool = ctx.enter_context(tc.tile_pool(name="vpool", bufs=V_SLOTS))
         loads = ctx.enter_context(tc.tile_pool(name="loads", bufs=3))
         rows = ctx.enter_context(tc.tile_pool(name="rows", bufs=2))
         packs = ctx.enter_context(tc.tile_pool(name="packs", bufs=2))
         small = ctx.enter_context(tc.tile_pool(name="small", bufs=2))
-        flipped = ctx.enter_context(tc.psum_pool(name="flipped", bufs=4))
+        flipped = ctx.enter_context(tc.psum_pool(name="flipped", bufs=2))
+        spread = ctx.enter_context(tc.psum_pool(name="spread", bufs=2))
         sums = ctx.enter_context(tc.psum_pool(name="sums", bufs=1))
 
         ident = const.tile([P, P], F32)
@@ -51,8 +54,25 @@ def tile_probprotoseghead_k_kernel(
         neg_half = const.tile([P, 1], F32)
         nc.vector.memset(neg_half[:], -0.5)
 
-        w_all = const.tile([P, K], BF16)
-        b_all = const.tile([P, K], BF16)
+        ident16 = const.tile([P, P], BF16)
+        make_identity(nc, ident16[:])
+        w_cols = const.tile([P, P], BF16)
+        b_cols = const.tile([P, P], BF16)
+        for vector, cols_tile in ((ln_w, w_cols), (ln_b, b_cols)):
+            as_rows = small.tile([P, P], BF16)
+            nc.sync.dma_start(out=as_rows[:], in_=vector.rearrange("(j p) -> j p", p=P))
+            turned = spread.tile([P, BANK_BF16], BF16, tag="gain")
+            nc.tensor.transpose(turned[:, 0:P], as_rows[:], ident16[:])
+            nc.vector.tensor_copy(out=cols_tile[:], in_=turned[:, 0:P])
+
+        def spread_over_partitions(cols_tile, first_k, tag):
+            bank = spread.tile([P, BANK_BF16], BF16, tag=tag)
+            for i in range(BANK_BF16 // P):
+                j = first_k // P + i
+                nc.tensor.transpose(
+                    bank[:, i * P : (i + 1) * P], cols_tile[:, j : j + 1].to_broadcast([P, P]), ident16[:]
+                )
+            return bank
 
         x_codes0 = const.tile([P, N_CHUNKS * WORDS_PER_CHUNK], U32, align_bytes=64)
         x_codes1 = const.tile([P, N_CHUNKS * WORDS_PER_CHUNK], U32, align_bytes=64)
@@ -66,7 +86,7 @@ def tile_probprotoseghead_k_kernel(
         xv_parts = const.tile([P, N_CHUNKS], F32)
         pv_parts = const.tile([P, N_CHUNKS], F32)
 
-        def quantise_rows(row16, codes, scales):
+        def quantise_rows(row16, codes, scales, copy_out):
             words = row16[:].bitcast(F32).rearrange(
                 "p (g q u) -> p g u q", g=PASSES_PER_CHUNK, u=2
             )
@@ -79,9 +99,7 @@ def tile_probprotoseghead_k_kernel(
                 for g in range(2):
                     for u in range(2):
                         nc.tensor.transpose(bank[:, g, u, :], words[:, 2 * h + g, u, :], ident[:])
-                nc.scalar.copy(
-                    out=grouped_words[:, h], in_=bank[:].rearrange("p g u n -> p g n u")
-                )
+                copy_out(out=grouped_words[:, h], in_=bank[:].rearrange("p g u n -> p g n u"))
             nc.vector.quantize_mx(out=codes.bitcast(FP8X4), scales=scales, in_=grouped[:])
 
         def cross_chunk(j):
@@ -97,7 +115,7 @@ def tile_probprotoseghead_k_kernel(
                 )
                 codes = packs.tile([P, WORDS_PER_CHUNK], U32, align_bytes=64, tag="codes")
                 scales = packs.tile([P, WORDS_PER_CHUNK], U8, align_bytes=64, tag="scales")
-                quantise_rows(std16, codes[:], scales[:])
+                quantise_rows(std16, codes[:], scales[:], nc.scalar.copy)
                 operands.append((codes, scales))
             (xc, xs), (pc, ps) = operands
             for g in range(PASSES_PER_CHUNK):
@@ -133,7 +151,7 @@ def tile_probprotoseghead_k_kernel(
                 nc.sync.dma_start(out=mean[:], in_=mean_rows[:, cols])
                 v = vpool.tile([P, CHUNK], F32)
                 nc.scalar.activation(out=v[:], in_=logvar[:], func=ACT.Exp, scale=0.5)
-                nc.vector.tensor_mul(out=v[:], in0=noise[:], in1=v[:])
+                nc.gpsimd.tensor_mul(out=v[:], in0=noise[:], in1=v[:])
                 nc.vector.scalar_tensor_tensor(
                     out=v[:], in0=v[:], scalar=1.0, in1=mean[:], op0=ALU.mult, op1=ALU.add,
                     accum_out=v_sum[:, c : c + 1],
@@ -148,11 +166,6 @@ def tile_probprotoseghead_k_kernel(
                     accum_out=v_sq[:, c : c + 1],
                 )
                 v_chunks.append(v)
-            if plane == 0:
-                for c in range(N_CHUNKS):
-                    cols = slice(c * CHUNK, (c + 1) * CHUNK)
-                    nc.sync.dma_start(out=w_all[:, cols], in_=ln_w[cols].partition_broadcast(P))
-                    nc.sync.dma_start(out=b_all[:, cols], in_=ln_b[cols].partition_broadcast(P))
 
             mu = small.tile([P, 1], F32)
             nc.vector.reduce_sum(out=mu[:], in_=v_sum[:], axis=AXIS_X)
@@ -171,15 +184,18 @@ def tile_probprotoseghead_k_kernel(
 
             u_sq = small.tile([P, N_CHUNKS], F32)
             for c, v in enumerate(v_chunks):
-                cols = slice(c * CHUNK, (c + 1) * CHUNK)
-                nc.vector.scalar_tensor_tensor(
-                    out=v[:], in0=v[:], scalar=mu[:], in1=w_all[:, cols],
-                    op0=ALU.subtract, op1=ALU.mult,
-                )
-                nc.vector.scalar_tensor_tensor(
-                    out=v[:], in0=v[:], scalar=rstd[:], in1=b_all[:, cols],
-                    op0=ALU.mult, op1=ALU.add,
-                )
+                for first in range(0, CHUNK, BANK_BF16):
+                    part = v[:, first : first + BANK_BF16]
+                    gain = spread_over_partitions(w_cols, c * CHUNK + first, "gain")
+                    nc.vector.scalar_tensor_tensor(
+                        out=part, in0=part, scalar=mu[:], in1=gain[:],
+                        op0=ALU.subtract, op1=ALU.mult,
+                    )
+                    bias = spread_over_partitions(b_cols, c * CHUNK + first, "bias")
+                    nc.vector.scalar_tensor_tensor(
+                        out=part, in0=part, scalar=rstd[:], in1=bias[:],
+                        op0=ALU.mult, op1=ALU.add,
+                    )
                 squares = rows.tile([P, CHUNK], BF16, tag="squares")
                 nc.scalar.activation(
                     out=squares[:], in_=v[:], func=ACT.Square, accum_out=u_sq[:, c : c + 1]
@@ -199,12 +215,13 @@ def tile_probprotoseghead_k_kernel(
                 nc.vector.tensor_scalar_mul(out=unit16[:], in0=v[:], scalar1=inv_norm[:])
                 if plane < SAMPLES:
                     quantise_rows(
-                        unit16, x_codes[plane][:, chunk_words], x_scales[plane][:, chunk_words]
+                        unit16, x_codes[plane][:, chunk_words], x_scales[plane][:, chunk_words],
+                        nc.vector.tensor_copy,
                     )
                     continue
                 p_codes = packs.tile([P, WORDS_PER_CHUNK], U32, align_bytes=64, tag="codes")
                 p_scales = packs.tile([P, WORDS_PER_CHUNK], U8, align_bytes=64, tag="scales")
-                quantise_rows(unit16, p_codes[:], p_scales[:])
+                quantise_rows(unit16, p_codes[:], p_scales[:], nc.vector.tensor_copy)
                 for g in range(PASSES_PER_CHUNK):
                     one = slice(g * P, (g + 1) * P)
                     x_one = slice(c * WORDS_PER_CHUNK + g * P, c * WORDS_PER_CHUNK + (g + 1) * P)
@@ -233,8 +250,9 @@ def tile_probprotoseghead_k_kernel(
         nc.vector.reduce_sum(out=pv_sum[:], in_=pv_parts[:], axis=AXIS_X)
         pv_repeated = small.tile([P, P], F32)
         nc.vector.tensor_scalar_mul(out=pv_repeated[:], in0=ones[:], scalar1=pv_sum[:])
-        pv_along = sums.tile([P, P], F32)
-        nc.tensor.transpose(pv_along[:], pv_repeated[:], ident[:])
+        pv_bank = flipped.tile([P, 2, 2, P], F32, tag="bank")
+        pv_along = pv_bank[:, 0, 0, :]
+        nc.tensor.transpose(pv_along, pv_repeated[:], ident[:])
 
         result = small.tile([P, P], F32)
         nc.vector.tensor_scalar(
@@ -242,7 +260,7 @@ def tile_probprotoseghead_k_kernel(
             op0=ALU.mult, op1=ALU.add,
         )
         nc.vector.scalar_tensor_tensor(
-            out=result[:], in0=pv_along[:], scalar=-LAMDA, in1=result[:],
+            out=result[:], in0=pv_along, scalar=-LAMDA, in1=result[:],
             op0=ALU.mult, op1=ALU.add,
         )
         nc.vector.scalar_tensor_tensor(

@@ -86,7 +86,7 @@ def tile_probprotoseghead_k_kernel(
         xv_parts = const.tile([P, N_CHUNKS], F32)
         pv_parts = const.tile([P, N_CHUNKS], F32)
 
-        def quantise_rows(row16, codes, scales, copy_out):
+        def quantise_rows(row16, codes, scales):
             words = row16[:].bitcast(F32).rearrange(
                 "p (g q u) -> p g u q", g=PASSES_PER_CHUNK, u=2
             )
@@ -99,7 +99,9 @@ def tile_probprotoseghead_k_kernel(
                 for g in range(2):
                     for u in range(2):
                         nc.tensor.transpose(bank[:, g, u, :], words[:, 2 * h + g, u, :], ident[:])
-                copy_out(out=grouped_words[:, h], in_=bank[:].rearrange("p g u n -> p g n u"))
+                nc.scalar.copy(
+                    out=grouped_words[:, h], in_=bank[:].rearrange("p g u n -> p g n u")
+                )
             nc.vector.quantize_mx(out=codes.bitcast(FP8X4), scales=scales, in_=grouped[:])
 
         def cross_chunk(j):
@@ -115,7 +117,7 @@ def tile_probprotoseghead_k_kernel(
                 )
                 codes = packs.tile([P, WORDS_PER_CHUNK], U32, align_bytes=64, tag="codes")
                 scales = packs.tile([P, WORDS_PER_CHUNK], U8, align_bytes=64, tag="scales")
-                quantise_rows(std16, codes[:], scales[:], nc.scalar.copy)
+                quantise_rows(std16, codes[:], scales[:])
                 operands.append((codes, scales))
             (xc, xs), (pc, ps) = operands
             for g in range(PASSES_PER_CHUNK):
@@ -151,7 +153,7 @@ def tile_probprotoseghead_k_kernel(
                 nc.sync.dma_start(out=mean[:], in_=mean_rows[:, cols])
                 v = vpool.tile([P, CHUNK], F32)
                 nc.scalar.activation(out=v[:], in_=logvar[:], func=ACT.Exp, scale=0.5)
-                nc.gpsimd.tensor_mul(out=v[:], in0=noise[:], in1=v[:])
+                nc.vector.tensor_mul(out=v[:], in0=noise[:], in1=v[:])
                 nc.vector.scalar_tensor_tensor(
                     out=v[:], in0=v[:], scalar=1.0, in1=mean[:], op0=ALU.mult, op1=ALU.add,
                     accum_out=v_sum[:, c : c + 1],
@@ -215,13 +217,12 @@ def tile_probprotoseghead_k_kernel(
                 nc.vector.tensor_scalar_mul(out=unit16[:], in0=v[:], scalar1=inv_norm[:])
                 if plane < SAMPLES:
                     quantise_rows(
-                        unit16, x_codes[plane][:, chunk_words], x_scales[plane][:, chunk_words],
-                        nc.vector.tensor_copy,
+                        unit16, x_codes[plane][:, chunk_words], x_scales[plane][:, chunk_words]
                     )
                     continue
                 p_codes = packs.tile([P, WORDS_PER_CHUNK], U32, align_bytes=64, tag="codes")
                 p_scales = packs.tile([P, WORDS_PER_CHUNK], U8, align_bytes=64, tag="scales")
-                quantise_rows(unit16, p_codes[:], p_scales[:], nc.vector.tensor_copy)
+                quantise_rows(unit16, p_codes[:], p_scales[:])
                 for g in range(PASSES_PER_CHUNK):
                     one = slice(g * P, (g + 1) * P)
                     x_one = slice(c * WORDS_PER_CHUNK + g * P, c * WORDS_PER_CHUNK + (g + 1) * P)

@@ -19,12 +19,12 @@ N_CHUNKS = K // CHUNK
 K_PASS = 512
 PASSES_PER_CHUNK = CHUNK // K_PASS
 WORDS_PER_CHUNK = PASSES_PER_CHUNK * P
+BANK_BF16 = 1024
 SAMPLES = 2
+FEATURES, PROTOTYPES = 0, 1
+CROSS_EVERY = 4
 LN_EPS = 1e-5
 LAMDA = 1.0 / (K // 4)
-CROSS_EVERY = 4
-BANK_BF16 = 1024
-V_SLOTS = 14
 
 FLOPS = 2 * (SAMPLES * P) * (SAMPLES * P) * K + 2 * P * P * K
 
@@ -35,44 +35,44 @@ def tile_probprotoseghead_k_kernel(
     nc = tc.nc
     proto_rows = prototypes.rearrange("c m k -> (c m) k")
     proto_var_rows = proto_var.rearrange("c m k -> (c m) k")
+    sides = [
+        (x, x_var, [eps_x[0], eps_x[1]]),
+        (
+            proto_rows,
+            proto_var_rows,
+            [eps_p[0].rearrange("c m k -> (c m) k"), eps_p[1].rearrange("c m k -> (c m) k")],
+        ),
+    ]
 
     with ExitStack() as ctx:
         const = ctx.enter_context(tc.tile_pool(name="const", bufs=1))
-        vpool = ctx.enter_context(tc.tile_pool(name="vpool", bufs=V_SLOTS))
+        vpool = ctx.enter_context(tc.tile_pool(name="vpool", bufs=2 * N_CHUNKS))
         loads = ctx.enter_context(tc.tile_pool(name="loads", bufs=3))
         rows = ctx.enter_context(tc.tile_pool(name="rows", bufs=2))
         packs = ctx.enter_context(tc.tile_pool(name="packs", bufs=2))
-        small = ctx.enter_context(tc.tile_pool(name="small", bufs=2))
+        stats = ctx.enter_context(tc.tile_pool(name="stats", bufs=2 * SAMPLES))
         flipped = ctx.enter_context(tc.psum_pool(name="flipped", bufs=2))
         spread = ctx.enter_context(tc.psum_pool(name="spread", bufs=2))
         sums = ctx.enter_context(tc.psum_pool(name="sums", bufs=1))
 
         ident = const.tile([P, P], F32)
         make_identity(nc, ident[:])
+        ident16 = const.tile([P, P], BF16)
+        make_identity(nc, ident16[:])
         ones = const.tile([P, P], F32)
         nc.vector.memset(ones[:], 1.0)
         neg_half = const.tile([P, 1], F32)
         nc.vector.memset(neg_half[:], -0.5)
 
-        ident16 = const.tile([P, P], BF16)
-        make_identity(nc, ident16[:])
+        w_rows = const.tile([P, P], BF16)
+        b_rows = const.tile([P, P], BF16)
         w_cols = const.tile([P, P], BF16)
         b_cols = const.tile([P, P], BF16)
-        for vector, cols_tile in ((ln_w, w_cols), (ln_b, b_cols)):
-            as_rows = small.tile([P, P], BF16)
+        for vector, as_rows, as_cols in ((ln_w, w_rows, w_cols), (ln_b, b_rows, b_cols)):
             nc.sync.dma_start(out=as_rows[:], in_=vector.rearrange("(j p) -> j p", p=P))
             turned = spread.tile([P, BANK_BF16], BF16, tag="gain")
             nc.tensor.transpose(turned[:, 0:P], as_rows[:], ident16[:])
-            nc.vector.tensor_copy(out=cols_tile[:], in_=turned[:, 0:P])
-
-        def spread_over_partitions(cols_tile, first_k, tag):
-            bank = spread.tile([P, BANK_BF16], BF16, tag=tag)
-            for i in range(BANK_BF16 // P):
-                j = first_k // P + i
-                nc.tensor.transpose(
-                    bank[:, i * P : (i + 1) * P], cols_tile[:, j : j + 1].to_broadcast([P, P]), ident16[:]
-                )
-            return bank
+            nc.vector.tensor_copy(out=as_cols[:], in_=turned[:, 0:P])
 
         x_codes0 = const.tile([P, N_CHUNKS * WORDS_PER_CHUNK], U32, align_bytes=64)
         x_codes1 = const.tile([P, N_CHUNKS * WORDS_PER_CHUNK], U32, align_bytes=64)
@@ -85,6 +85,15 @@ def tile_probprotoseghead_k_kernel(
         cross_sum = sums.tile([P, P], F32)
         xv_parts = const.tile([P, N_CHUNKS], F32)
         pv_parts = const.tile([P, N_CHUNKS], F32)
+
+        def spread_over_partitions(as_cols, first_k, tag):
+            bank = spread.tile([P, BANK_BF16], BF16, tag=tag)
+            for i in range(BANK_BF16 // P):
+                j = first_k // P + i
+                nc.tensor.transpose(
+                    bank[:, i * P : (i + 1) * P], as_cols[:, j : j + 1].to_broadcast([P, P]), ident16[:]
+                )
+            return bank
 
         def quantise_rows(row16, codes, scales):
             words = row16[:].bitcast(F32).rearrange(
@@ -108,7 +117,7 @@ def tile_probprotoseghead_k_kernel(
             cols = slice(j * CHUNK, (j + 1) * CHUNK)
             operands = []
             for logvar_rows, parts in ((x_var, xv_parts), (proto_var_rows, pv_parts)):
-                logvar = loads.tile([P, CHUNK], BF16, tag="logvar")
+                logvar = loads.tile([P, CHUNK], BF16, tag="logvar", bufs=3)
                 nc.sync.dma_start(out=logvar[:], in_=logvar_rows[:, cols])
                 std16 = rows.tile([P, CHUNK], BF16, tag="row16")
                 nc.scalar.activation(out=std16[:], in_=logvar[:], func=ACT.Exp, scale=0.5)
@@ -132,130 +141,189 @@ def tile_probprotoseghead_k_kernel(
                     stop=(j == N_CHUNKS - 1 and g == PASSES_PER_CHUNK - 1),
                 )
 
-        planes = [
-            (x, x_var, eps_x[0]),
-            (x, x_var, eps_x[1]),
-            (proto_rows, proto_var_rows, eps_p[0].rearrange("c m k -> (c m) k")),
-            (proto_rows, proto_var_rows, eps_p[1].rearrange("c m k -> (c m) k")),
-        ]
-        for plane, (mean_rows, logvar_rows, noise_rows) in enumerate(planes):
-            v_chunks = []
-            v_sum = small.tile([P, N_CHUNKS], F32)
-            v_sq = small.tile([P, N_CHUNKS], F32)
-            neg_shift = small.tile([P, 1], F32)
-            for c in range(N_CHUNKS):
-                cols = slice(c * CHUNK, (c + 1) * CHUNK)
-                logvar = loads.tile([P, CHUNK], BF16, tag="logvar")
-                nc.sync.dma_start(out=logvar[:], in_=logvar_rows[:, cols])
-                noise = loads.tile([P, CHUNK], BF16)
-                nc.sync.dma_start(out=noise[:], in_=noise_rows[:, cols])
-                mean = loads.tile([P, CHUNK], BF16)
-                nc.sync.dma_start(out=mean[:], in_=mean_rows[:, cols])
-                v = vpool.tile([P, CHUNK], F32)
-                nc.scalar.activation(out=v[:], in_=logvar[:], func=ACT.Exp, scale=0.5)
-                nc.vector.tensor_mul(out=v[:], in0=noise[:], in1=v[:])
+        def phase1_chunk(side, c):
+            mean_rows, logvar_rows, noise_rows = sides[side]
+            cols = slice(c * CHUNK, (c + 1) * CHUNK)
+            logvar = loads.tile([P, CHUNK], BF16, tag="logvar", bufs=3)
+            nc.sync.dma_start(out=logvar[:], in_=logvar_rows[:, cols])
+            noises = []
+            for sample in range(SAMPLES):
+                noise = loads.tile([P, CHUNK], BF16, tag="noise", bufs=4)
+                nc.sync.dma_start(out=noise[:], in_=noise_rows[sample][:, cols])
+                noises.append(noise)
+            mean = loads.tile([P, CHUNK], BF16, tag="mean", bufs=2)
+            nc.sync.dma_start(out=mean[:], in_=mean_rows[:, cols])
+            v0 = vpool.tile([P, CHUNK], F32, tag="v")
+            v1 = vpool.tile([P, CHUNK], F32, tag="v")
+            nc.scalar.activation(out=v0[:], in_=logvar[:], func=ACT.Exp, scale=0.5)
+            nc.vector.tensor_mul(out=v1[:], in0=noises[1][:], in1=v0[:])
+            nc.vector.tensor_mul(out=v0[:], in0=noises[0][:], in1=v0[:])
+            for sample, v in ((1, v1), (0, v0)):
+                kept = held[side][sample]
                 nc.vector.scalar_tensor_tensor(
                     out=v[:], in0=v[:], scalar=1.0, in1=mean[:], op0=ALU.mult, op1=ALU.add,
-                    accum_out=v_sum[:, c : c + 1],
+                    accum_out=kept["v_sum"][:, c : c + 1],
                 )
                 if c == 0:
                     nc.vector.tensor_scalar_mul(
-                        out=neg_shift[:], in0=v_sum[:, 0:1], scalar1=-1.0 / CHUNK
+                        out=kept["neg_shift"][:], in0=kept["v_sum"][:, 0:1], scalar1=-1.0 / CHUNK
                     )
                 squares = rows.tile([P, CHUNK], BF16, tag="squares")
                 nc.scalar.activation(
-                    out=squares[:], in_=v[:], func=ACT.Square, bias=neg_shift[:],
-                    accum_out=v_sq[:, c : c + 1],
+                    out=squares[:], in_=v[:], func=ACT.Square, bias=kept["neg_shift"][:],
+                    accum_out=kept["v_sq"][:, c : c + 1],
                 )
-                v_chunks.append(v)
+                kept["chunks"].append(v)
 
-            mu = small.tile([P, 1], F32)
-            nc.vector.reduce_sum(out=mu[:], in_=v_sum[:], axis=AXIS_X)
+        def layer_norm_statistics(kept):
+            mu = stats.tile([P, 1], F32)
+            nc.vector.reduce_sum(out=mu[:], in_=kept["v_sum"][:], axis=AXIS_X)
             nc.vector.tensor_scalar_mul(out=mu[:], in0=mu[:], scalar1=1.0 / K)
-            off = small.tile([P, 1], F32)
-            nc.vector.tensor_add(out=off[:], in0=mu[:], in1=neg_shift[:])
+            off = stats.tile([P, 1], F32)
+            nc.vector.tensor_add(out=off[:], in0=mu[:], in1=kept["neg_shift"][:])
             nc.vector.tensor_mul(out=off[:], in0=off[:], in1=off[:])
-            var = small.tile([P, 1], F32)
-            nc.vector.reduce_sum(out=var[:], in_=v_sq[:], axis=AXIS_X)
+            var = stats.tile([P, 1], F32)
+            nc.vector.reduce_sum(out=var[:], in_=kept["v_sq"][:], axis=AXIS_X)
             nc.vector.scalar_tensor_tensor(
                 out=var[:], in0=var[:], scalar=1.0 / K, in1=off[:], op0=ALU.mult, op1=ALU.subtract
             )
             nc.vector.tensor_scalar_add(out=var[:], in0=var[:], scalar1=LN_EPS)
-            rstd = small.tile([P, 1], F32)
+            rstd = stats.tile([P, 1], F32)
             nc.gpsimd.tensor_tensor(out=rstd[:], in0=var[:], in1=neg_half[:], op=ALU.pow)
+            kept["mu"] = mu
+            kept["rstd"] = rstd
 
-            u_sq = small.tile([P, N_CHUNKS], F32)
-            for c, v in enumerate(v_chunks):
-                for first in range(0, CHUNK, BANK_BF16):
-                    part = v[:, first : first + BANK_BF16]
-                    gain = spread_over_partitions(w_cols, c * CHUNK + first, "gain")
-                    nc.vector.scalar_tensor_tensor(
-                        out=part, in0=part, scalar=mu[:], in1=gain[:],
-                        op0=ALU.subtract, op1=ALU.mult,
-                    )
-                    bias = spread_over_partitions(b_cols, c * CHUNK + first, "bias")
-                    nc.vector.scalar_tensor_tensor(
-                        out=part, in0=part, scalar=rstd[:], in1=bias[:],
-                        op0=ALU.mult, op1=ALU.add,
-                    )
-                squares = rows.tile([P, CHUNK], BF16, tag="squares")
-                nc.scalar.activation(
-                    out=squares[:], in_=v[:], func=ACT.Square, accum_out=u_sq[:, c : c + 1]
+        def phase2_chunk(kept, c):
+            v = kept["chunks"][c]
+            halves = range(0, CHUNK, BANK_BF16)
+            for first in halves:
+                part = v[:, first : first + BANK_BF16]
+                gain = spread_over_partitions(w_cols, c * CHUNK + first, "gain")
+                nc.vector.scalar_tensor_tensor(
+                    out=part, in0=part, scalar=kept["mu"][:], in1=gain[:],
+                    op0=ALU.subtract, op1=ALU.mult,
                 )
-                if c % CROSS_EVERY == 0:
-                    cross_chunk(plane * (N_CHUNKS // CROSS_EVERY) + c // CROSS_EVERY)
+            for first in halves:
+                part = v[:, first : first + BANK_BF16]
+                bias = spread_over_partitions(b_cols, c * CHUNK + first, "bias")
+                nc.vector.scalar_tensor_tensor(
+                    out=part, in0=part, scalar=kept["rstd"][:], in1=bias[:],
+                    op0=ALU.mult, op1=ALU.add,
+                )
+            squares = rows.tile([P, CHUNK], BF16, tag="squares")
+            nc.scalar.activation(
+                out=squares[:], in_=v[:], func=ACT.Square, accum_out=kept["u_sq"][:, c : c + 1]
+            )
 
-            norm2 = small.tile([P, 1], F32)
-            nc.vector.reduce_sum(out=norm2[:], in_=u_sq[:], axis=AXIS_X)
+        def l2_norm_statistics(kept):
+            norm2 = stats.tile([P, 1], F32)
+            nc.vector.reduce_sum(out=norm2[:], in_=kept["u_sq"][:], axis=AXIS_X)
             nc.vector.tensor_scalar_max(out=norm2[:], in0=norm2[:], scalar1=1e-24)
-            inv_norm = small.tile([P, 1], F32)
+            inv_norm = stats.tile([P, 1], F32)
             nc.gpsimd.tensor_tensor(out=inv_norm[:], in0=norm2[:], in1=neg_half[:], op=ALU.pow)
+            kept["inv_norm"] = inv_norm
 
-            for c, v in enumerate(v_chunks):
-                chunk_words = slice(c * WORDS_PER_CHUNK, (c + 1) * WORDS_PER_CHUNK)
-                unit16 = rows.tile([P, CHUNK], BF16, tag="row16")
-                nc.vector.tensor_scalar_mul(out=unit16[:], in0=v[:], scalar1=inv_norm[:])
-                if plane < SAMPLES:
-                    quantise_rows(
-                        unit16, x_codes[plane][:, chunk_words], x_scales[plane][:, chunk_words]
+        def phase3_chunk(side, sample, c):
+            kept = held[side][sample]
+            chunk_words = slice(c * WORDS_PER_CHUNK, (c + 1) * WORDS_PER_CHUNK)
+            unit16 = rows.tile([P, CHUNK], BF16, tag="row16")
+            if side == FEATURES and sample == 1:
+                nc.scalar.activation(
+                    out=unit16[:], in_=kept["chunks"][c][:], func=ACT.Copy, scale=kept["inv_norm"][:]
+                )
+            else:
+                nc.vector.tensor_scalar_mul(
+                    out=unit16[:], in0=kept["chunks"][c][:], scalar1=kept["inv_norm"][:]
+                )
+            if side == FEATURES:
+                quantise_rows(
+                    unit16, x_codes[sample][:, chunk_words], x_scales[sample][:, chunk_words]
+                )
+                return
+            p_codes = packs.tile([P, WORDS_PER_CHUNK], U32, align_bytes=64, tag="codes")
+            p_scales = packs.tile([P, WORDS_PER_CHUNK], U8, align_bytes=64, tag="scales")
+            quantise_rows(unit16, p_codes[:], p_scales[:])
+            for g in range(PASSES_PER_CHUNK):
+                one = slice(g * P, (g + 1) * P)
+                x_one = slice(c * WORDS_PER_CHUNK + g * P, c * WORDS_PER_CHUNK + (g + 1) * P)
+                for r in range(SAMPLES):
+                    nc.tensor.matmul_mx(
+                        out=sim_sum[:],
+                        lhsT=x_codes[r][:, x_one].bitcast(FP8X4),
+                        lhsT_scale=x_scales[r][:, x_one],
+                        rhs=p_codes[:, one].bitcast(FP8X4),
+                        rhs_scale=p_scales[:, one],
+                        start=(sample == 0 and c == 0 and g == 0 and r == 0),
+                        stop=(
+                            sample == SAMPLES - 1
+                            and c == N_CHUNKS - 1
+                            and g == PASSES_PER_CHUNK - 1
+                            and r == SAMPLES - 1
+                        ),
                     )
-                    continue
-                p_codes = packs.tile([P, WORDS_PER_CHUNK], U32, align_bytes=64, tag="codes")
-                p_scales = packs.tile([P, WORDS_PER_CHUNK], U8, align_bytes=64, tag="scales")
-                quantise_rows(unit16, p_codes[:], p_scales[:])
-                for g in range(PASSES_PER_CHUNK):
-                    one = slice(g * P, (g + 1) * P)
-                    x_one = slice(c * WORDS_PER_CHUNK + g * P, c * WORDS_PER_CHUNK + (g + 1) * P)
-                    for r in range(SAMPLES):
-                        nc.tensor.matmul_mx(
-                            out=sim_sum[:],
-                            lhsT=x_codes[r][:, x_one].bitcast(FP8X4),
-                            lhsT_scale=x_scales[r][:, x_one],
-                            rhs=p_codes[:, one].bitcast(FP8X4),
-                            rhs_scale=p_scales[:, one],
-                            start=(plane == SAMPLES and c == 0 and g == 0 and r == 0),
-                            stop=(
-                                plane == 2 * SAMPLES - 1
-                                and c == N_CHUNKS - 1
-                                and g == PASSES_PER_CHUNK - 1
-                                and r == SAMPLES - 1
-                            ),
-                        )
 
-        xv_term = small.tile([P, 1], F32)
+        held = []
+        for side in (FEATURES, PROTOTYPES):
+            held.append([])
+            for sample in range(SAMPLES):
+                v_sum = stats.tile([P, N_CHUNKS], F32)
+                v_sq = stats.tile([P, N_CHUNKS], F32)
+                u_sq = stats.tile([P, N_CHUNKS], F32)
+                neg_shift = stats.tile([P, 1], F32)
+                held[side].append(
+                    {"v_sum": v_sum, "v_sq": v_sq, "u_sq": u_sq, "neg_shift": neg_shift, "chunks": []}
+                )
+
+        cross_done = []
+
+        def next_cross_chunk():
+            cross_chunk(len(cross_done))
+            cross_done.append(len(cross_done))
+
+        for c in range(N_CHUNKS):
+            phase1_chunk(FEATURES, c)
+        for kept in held[FEATURES]:
+            layer_norm_statistics(kept)
+        for kept in held[FEATURES]:
+            for c in range(N_CHUNKS):
+                phase2_chunk(kept, c)
+                if c % CROSS_EVERY == 1:
+                    next_cross_chunk()
+            l2_norm_statistics(kept)
+        for c in range(N_CHUNKS):
+            for sample in range(SAMPLES):
+                phase3_chunk(FEATURES, sample, c)
+            phase1_chunk(PROTOTYPES, c)
+        for kept in held[PROTOTYPES]:
+            layer_norm_statistics(kept)
+        for c in range(N_CHUNKS):
+            phase2_chunk(held[PROTOTYPES][0], c)
+            if c % CROSS_EVERY == 1:
+                next_cross_chunk()
+        l2_norm_statistics(held[PROTOTYPES][0])
+        for c in range(N_CHUNKS):
+            phase3_chunk(PROTOTYPES, 0, c)
+            phase2_chunk(held[PROTOTYPES][1], c)
+            if c % CROSS_EVERY == 1:
+                next_cross_chunk()
+        l2_norm_statistics(held[PROTOTYPES][1])
+        for c in range(N_CHUNKS):
+            phase3_chunk(PROTOTYPES, 1, c)
+
+        xv_term = const.tile([P, 1], F32)
         nc.vector.reduce_sum(out=xv_term[:], in_=xv_parts[:], axis=AXIS_X)
         nc.vector.tensor_scalar(
             out=xv_term[:], in0=xv_term[:], scalar1=-LAMDA, scalar2=-2.0, op0=ALU.mult, op1=ALU.add
         )
-        pv_sum = small.tile([P, 1], F32)
+        pv_sum = const.tile([P, 1], F32)
         nc.vector.reduce_sum(out=pv_sum[:], in_=pv_parts[:], axis=AXIS_X)
-        pv_repeated = small.tile([P, P], F32)
+        pv_repeated = const.tile([P, P], F32)
         nc.vector.tensor_scalar_mul(out=pv_repeated[:], in0=ones[:], scalar1=pv_sum[:])
         pv_bank = flipped.tile([P, 2, 2, P], F32, tag="bank")
         pv_along = pv_bank[:, 0, 0, :]
         nc.tensor.transpose(pv_along, pv_repeated[:], ident[:])
 
-        result = small.tile([P, P], F32)
+        result = const.tile([P, P], F32)
         nc.vector.tensor_scalar(
             out=result[:], in0=cross_sum[:], scalar1=2.0 * LAMDA, scalar2=xv_term[:],
             op0=ALU.mult, op1=ALU.add,

@@ -19,7 +19,9 @@ N_CHUNKS = K // CHUNK
 K_PASS = 512
 PASSES_PER_CHUNK = CHUNK // K_PASS
 WORDS_PER_CHUNK = PASSES_PER_CHUNK * P
-BANK_BF16 = 1024
+BANK_WORDS = 512
+BANK_BF16 = 2 * BANK_WORDS
+BIAS_COLUMN = K // (2 * P)
 SAMPLES = 2
 FEATURES, PROTOTYPES = 0, 1
 CROSS_EVERY = 4
@@ -57,22 +59,18 @@ def tile_probprotoseghead_k_kernel(
 
         ident = const.tile([P, P], F32)
         make_identity(nc, ident[:])
-        ident16 = const.tile([P, P], BF16)
-        make_identity(nc, ident16[:])
         ones = const.tile([P, P], F32)
         nc.vector.memset(ones[:], 1.0)
         neg_half = const.tile([P, 1], F32)
         nc.vector.memset(neg_half[:], -0.5)
 
-        w_rows = const.tile([P, P], BF16)
-        b_rows = const.tile([P, P], BF16)
-        w_cols = const.tile([P, P], BF16)
-        b_cols = const.tile([P, P], BF16)
-        for vector, as_rows, as_cols in ((ln_w, w_rows, w_cols), (ln_b, b_rows, b_cols)):
-            nc.sync.dma_start(out=as_rows[:], in_=vector.rearrange("(j p) -> j p", p=P))
-            turned = spread.tile([P, BANK_BF16], BF16, tag="gain")
-            nc.tensor.transpose(turned[:, 0:P], as_rows[:], ident16[:])
-            nc.vector.tensor_copy(out=as_cols[:], in_=turned[:, 0:P])
+        wb_rows = const.tile([P, 2 * P], BF16)
+        nc.sync.dma_start(out=wb_rows[0:BIAS_COLUMN, :], in_=ln_w.rearrange("(j c) -> j c", c=2 * P))
+        nc.sync.dma_start(out=wb_rows[BIAS_COLUMN:P, :], in_=ln_b.rearrange("(j c) -> j c", c=2 * P))
+        turned = spread.tile([P, BANK_WORDS], F32, tag="gain")
+        nc.tensor.transpose(turned[:, 0:P], wb_rows[:].bitcast(F32), ident[:])
+        wb_cols = const.tile([P, P], F32)
+        nc.vector.tensor_copy(out=wb_cols[:], in_=turned[:, 0:P])
 
         x_codes0 = const.tile([P, N_CHUNKS * WORDS_PER_CHUNK], U32, align_bytes=64)
         x_codes1 = const.tile([P, N_CHUNKS * WORDS_PER_CHUNK], U32, align_bytes=64)
@@ -86,14 +84,14 @@ def tile_probprotoseghead_k_kernel(
         xv_parts = const.tile([P, N_CHUNKS], F32)
         pv_parts = const.tile([P, N_CHUNKS], F32)
 
-        def spread_over_partitions(as_cols, first_k, tag):
-            bank = spread.tile([P, BANK_BF16], BF16, tag=tag)
-            for i in range(BANK_BF16 // P):
-                j = first_k // P + i
+        def spread_over_partitions(first_column, tag):
+            bank = spread.tile([P, BANK_WORDS], F32, tag=tag)
+            for i in range(BANK_WORDS // P):
+                j = first_column + i
                 nc.tensor.transpose(
-                    bank[:, i * P : (i + 1) * P], as_cols[:, j : j + 1].to_broadcast([P, P]), ident16[:]
+                    bank[:, i * P : (i + 1) * P], wb_cols[:, j : j + 1].to_broadcast([P, P]), ident[:]
                 )
-            return bank
+            return bank[:].bitcast(BF16)
 
         def quantise_rows(row16, codes, scales):
             words = row16[:].bitcast(F32).rearrange(
@@ -198,16 +196,16 @@ def tile_probprotoseghead_k_kernel(
             halves = range(0, CHUNK, BANK_BF16)
             for first in halves:
                 part = v[:, first : first + BANK_BF16]
-                gain = spread_over_partitions(w_cols, c * CHUNK + first, "gain")
+                gain = spread_over_partitions((c * CHUNK + first) // (2 * P), "gain")
                 nc.vector.scalar_tensor_tensor(
-                    out=part, in0=part, scalar=kept["mu"][:], in1=gain[:],
+                    out=part, in0=part, scalar=kept["mu"][:], in1=gain,
                     op0=ALU.subtract, op1=ALU.mult,
                 )
             for first in halves:
                 part = v[:, first : first + BANK_BF16]
-                bias = spread_over_partitions(b_cols, c * CHUNK + first, "bias")
+                bias = spread_over_partitions(BIAS_COLUMN + (c * CHUNK + first) // (2 * P), "bias")
                 nc.vector.scalar_tensor_tensor(
-                    out=part, in0=part, scalar=kept["rstd"][:], in1=bias[:],
+                    out=part, in0=part, scalar=kept["rstd"][:], in1=bias,
                     op0=ALU.mult, op1=ALU.add,
                 )
             squares = rows.tile([P, CHUNK], BF16, tag="squares")

@@ -95,7 +95,7 @@ def tile_probprotoseghead_k_kernel(
 
         def quantise_rows(row16, codes, scales):
             words = row16[:].bitcast(F32).rearrange(
-                "p (g q u) -> p g u q", g=PASSES_PER_CHUNK, u=2
+                "p (g u q) -> p g u q", g=PASSES_PER_CHUNK, u=2
             )
             grouped = packs.tile([P, CHUNK], BF16, align_bytes=64)
             grouped_words = grouped[:].bitcast(F32).rearrange(

@@ -229,6 +229,11 @@ def tile_probprotoseghead_k_kernel(
                 nc.scalar.activation(
                     out=unit16[:], in_=kept["chunks"][c][:], func=ACT.Copy, scale=kept["inv_norm"][:]
                 )
+            elif side == PROTOTYPES and sample == 0:
+                nc.gpsimd.tensor_scalar(
+                    out=unit16[:], in0=kept["chunks"][c][:], scalar1=kept["inv_norm"][:], scalar2=0.0,
+                    op0=ALU.mult, op1=ALU.add,
+                )
             else:
                 nc.vector.tensor_scalar_mul(
                     out=unit16[:], in0=kept["chunks"][c][:], scalar1=kept["inv_norm"][:]

@@ -24,7 +24,16 @@ BANK_BF16 = 2 * BANK_WORDS
 BIAS_COLUMN = K // (2 * P)
 SAMPLES = 2
 FEATURES, PROTOTYPES = 0, 1
-CROSS_EVERY = 4
+CROSS_ORDER = [(side, j) for j in (0, 1, 7, 6, 2, 3, 4, 5) for side in (0, 1)]
+PIECES = {
+    1: (0, 1, 1, 1, 1, 0, 0, 0, 0),
+    2: (1, 1, 1, 1, 1, 1, 0, 0),
+    3: (1, 1, 1, 1, 1, 1, 0, 0, 0),
+    4: (0, 0, 1, 1, 0, 0, 0, 0, 0),
+    5: (1, 1, 1, 1, 1, 1, 0, 0),
+    6: (1, 1, 1, 1, 1, 1, 0, 0, 0),
+    7: (1, 1, 1, 1, 1, 1, 0, 0, 0, 0),
+}
 LN_EPS = 1e-5
 LAMDA = 1.0 / (K // 4)
 
@@ -48,7 +57,7 @@ def tile_probprotoseghead_k_kernel(
 
     with ExitStack() as ctx:
         const = ctx.enter_context(tc.tile_pool(name="const", bufs=1))
-        vpool = ctx.enter_context(tc.tile_pool(name="vpool", bufs=2 * N_CHUNKS))
+        vpool = ctx.enter_context(tc.tile_pool(name="vpool", bufs=N_CHUNKS))
         loads = ctx.enter_context(tc.tile_pool(name="loads", bufs=3))
         rows = ctx.enter_context(tc.tile_pool(name="rows", bufs=2))
         packs = ctx.enter_context(tc.tile_pool(name="packs", bufs=2))
@@ -59,25 +68,14 @@ def tile_probprotoseghead_k_kernel(
 
         ident = const.tile([P, P], F32)
         make_identity(nc, ident[:])
-        ones = const.tile([P, P], F32)
-        nc.vector.memset(ones[:], 1.0)
         neg_half = const.tile([P, 1], F32)
         nc.vector.memset(neg_half[:], -0.5)
 
-        wb_rows = const.tile([P, 2 * P], BF16)
-        nc.sync.dma_start(out=wb_rows[0:BIAS_COLUMN, :], in_=ln_w.rearrange("(j c) -> j c", c=2 * P))
-        nc.sync.dma_start(out=wb_rows[BIAS_COLUMN:P, :], in_=ln_b.rearrange("(j c) -> j c", c=2 * P))
-        turned = spread.tile([P, BANK_WORDS], F32, tag="gain")
-        nc.tensor.transpose(turned[:, 0:P], wb_rows[:].bitcast(F32), ident[:])
-        wb_cols = const.tile([P, P], F32)
-        nc.vector.tensor_copy(out=wb_cols[:], in_=turned[:, 0:P])
-
         x_codes0 = const.tile([P, N_CHUNKS * WORDS_PER_CHUNK], U32, align_bytes=64)
         x_codes1 = const.tile([P, N_CHUNKS * WORDS_PER_CHUNK], U32, align_bytes=64)
-        x_scales0 = const.tile([P, N_CHUNKS * WORDS_PER_CHUNK], U8, align_bytes=64)
-        x_scales1 = const.tile([P, N_CHUNKS * WORDS_PER_CHUNK], U8, align_bytes=64)
+        x_planes = const.tile([P, N_CHUNKS * WORDS_PER_CHUNK], U8, align_bytes=64)
         x_codes = [x_codes0, x_codes1]
-        x_scales = [x_scales0, x_scales1]
+        x_scales = [x_planes[0:P, :], x_planes[4:P, :]]
 
         sim_sum = sums.tile([P, P], F32)
         cross_sum = sums.tile([P, P], F32)
@@ -93,11 +91,11 @@ def tile_probprotoseghead_k_kernel(
                 )
             return bank[:].bitcast(BF16)
 
-        def quantise_rows(row16, codes, scales):
+        def turn_rows(row16, copies):
             words = row16[:].bitcast(F32).rearrange(
                 "p (g u q) -> p g u q", g=PASSES_PER_CHUNK, u=2
             )
-            grouped = packs.tile([P, CHUNK], BF16, align_bytes=64)
+            grouped = packs.tile([P, CHUNK], BF16, tag="grouped", bufs=3, align_bytes=64)
             grouped_words = grouped[:].bitcast(F32).rearrange(
                 "p (h g n u) -> p h g n u", h=PASSES_PER_CHUNK // 2, g=2, u=2
             )
@@ -106,146 +104,186 @@ def tile_probprotoseghead_k_kernel(
                 for g in range(2):
                     for u in range(2):
                         nc.tensor.transpose(bank[:, g, u, :], words[:, 2 * h + g, u, :], ident[:])
-                nc.scalar.copy(
+                copies[h](
                     out=grouped_words[:, h], in_=bank[:].rearrange("p g u n -> p g n u")
                 )
+            return grouped
+
+        def quantise(grouped, codes, scales):
             nc.vector.quantize_mx(out=codes.bitcast(FP8X4), scales=scales, in_=grouped[:])
 
-        def cross_chunk(j):
-            cols = slice(j * CHUNK, (j + 1) * CHUNK)
-            operands = []
-            for logvar_rows, parts in ((x_var, xv_parts), (proto_var_rows, pv_parts)):
-                logvar = loads.tile([P, CHUNK], BF16, tag="logvar", bufs=3)
-                nc.sync.dma_start(out=logvar[:], in_=logvar_rows[:, cols])
-                std16 = rows.tile([P, CHUNK], BF16, tag="row16")
-                nc.scalar.activation(out=std16[:], in_=logvar[:], func=ACT.Exp, scale=0.5)
-                nc.scalar.activation(
-                    out=logvar[:], in_=logvar[:], func=ACT.Exp, accum_out=parts[:, j : j + 1]
-                )
-                codes = packs.tile([P, WORDS_PER_CHUNK], U32, align_bytes=64, tag="codes")
-                scales = packs.tile([P, WORDS_PER_CHUNK], U8, align_bytes=64, tag="scales")
-                quantise_rows(std16, codes[:], scales[:])
-                operands.append((codes, scales))
-            (xc, xs), (pc, ps) = operands
-            for g in range(PASSES_PER_CHUNK):
-                one = slice(g * P, (g + 1) * P)
-                nc.tensor.matmul_mx(
-                    out=cross_sum[:],
-                    lhsT=xc[:, one].bitcast(FP8X4),
-                    lhsT_scale=xs[:, one],
-                    rhs=pc[:, one].bitcast(FP8X4),
-                    rhs_scale=ps[:, one],
-                    start=(j == 0 and g == 0),
-                    stop=(j == N_CHUNKS - 1 and g == PASSES_PER_CHUNK - 1),
-                )
+        wb_rows = const.tile([P, 2 * P], BF16)
+        wb_cols = const.tile([P, P], F32)
 
-        def phase1_chunk(side, c):
-            mean_rows, logvar_rows, noise_rows = sides[side]
-            cols = slice(c * CHUNK, (c + 1) * CHUNK)
-            logvar = loads.tile([P, CHUNK], BF16, tag="logvar", bufs=3)
-            nc.sync.dma_start(out=logvar[:], in_=logvar_rows[:, cols])
-            noises = []
-            for sample in range(SAMPLES):
-                noise = loads.tile([P, CHUNK], BF16, tag="noise", bufs=4)
-                nc.sync.dma_start(out=noise[:], in_=noise_rows[sample][:, cols])
-                noises.append(noise)
-            mean = loads.tile([P, CHUNK], BF16, tag="mean", bufs=2)
-            nc.sync.dma_start(out=mean[:], in_=mean_rows[:, cols])
-            v0 = vpool.tile([P, CHUNK], F32, tag="v")
-            v1 = vpool.tile([P, CHUNK], F32, tag="v")
-            nc.scalar.activation(out=v0[:], in_=logvar[:], func=ACT.Exp, scale=0.5)
-            nc.vector.tensor_mul(out=v1[:], in0=noises[1][:], in1=v0[:])
-            nc.vector.tensor_mul(out=v0[:], in0=noises[0][:], in1=v0[:])
-            for sample, v in ((1, v1), (0, v0)):
-                kept = held[side][sample]
-                nc.vector.scalar_tensor_tensor(
-                    out=v[:], in0=v[:], scalar=1.0, in1=mean[:], op0=ALU.mult, op1=ALU.add,
-                    accum_out=kept["v_sum"][:, c : c + 1],
+        def load_gain_and_bias():
+            nc.sync.dma_start(out=wb_rows[0:BIAS_COLUMN, :], in_=ln_w.rearrange("(j c) -> j c", c=2 * P))
+            nc.sync.dma_start(out=wb_rows[BIAS_COLUMN:P, :], in_=ln_b.rearrange("(j c) -> j c", c=2 * P))
+
+        def turn_gain_and_bias():
+            turned = spread.tile([P, BANK_WORDS], F32, tag="gain")
+            nc.tensor.transpose(turned[:, 0:P], wb_rows[:].bitcast(F32), ident[:])
+            nc.vector.tensor_copy(out=wb_cols[:], in_=turned[:, 0:P])
+
+        def load(rows_in_hbm, c, tag, bufs):
+            tile = loads.tile([P, CHUNK], BF16, tag=tag, bufs=bufs)
+            nc.sync.dma_start(out=tile[:], in_=rows_in_hbm[:, c * CHUNK : (c + 1) * CHUNK])
+            return tile
+
+        def load_logvar(unit, c):
+            if inside(c):
+                unit["logvars"].append(load(unit["logvar"], c, "logvar", 2))
+
+        def load_noise(unit, c):
+            if inside(c):
+                unit["noises"].append(load(unit["noise"], c, "noise", 3))
+
+        def load_mean(unit, c):
+            if inside(c):
+                unit["means"].append(load(unit["mean"], c, "mean", 2))
+
+        def square_sum(values, bias, total):
+            squares = loads.tile([P, CHUNK], BF16, tag="squares", bufs=1)
+            nc.scalar.activation(
+                out=squares[:], in_=values[:], func=ACT.Square, bias=bias, accum_out=total
+            )
+
+        gate = const.tile([P, 1], F32)
+        live_std = {}
+
+        def phase1_std(unit, c):
+            if not inside(c):
+                return
+            chunk = vpool.tile([P, CHUNK], F32, tag="v1")
+            nc.scalar.activation(out=chunk[:], in_=unit["logvars"][c][:], func=ACT.Exp, scale=0.5)
+            unit["chunks"].append(chunk)
+            live_std[(unit["side"], c)] = chunk
+
+        def phase1_first(unit, other, c):
+            chunk = vpool.tile([P, CHUNK], F32, tag="v0")
+            for part in halves if unit["side"] == FEATURES and c == 0 else (slice(0, CHUNK),):
+                nc.vector.tensor_mul(
+                    out=chunk[:, part], in0=unit["noises"][c][:, part], in1=other["chunks"][c][:, part]
                 )
-                if c == 0:
-                    nc.vector.tensor_scalar_mul(
-                        out=kept["neg_shift"][:], in0=kept["v_sum"][:, 0:1], scalar1=-1.0 / CHUNK
-                    )
-                squares = rows.tile([P, CHUNK], BF16, tag="squares")
-                nc.scalar.activation(
-                    out=squares[:], in_=v[:], func=ACT.Square, bias=kept["neg_shift"][:],
-                    accum_out=kept["v_sq"][:, c : c + 1],
+            unit["chunks"].append(chunk)
+
+        def phase1_second(unit, c):
+            chunk = unit["chunks"][c]
+            live_std[(unit["side"], c)] = None
+            if c > 0:
+                nc.gpsimd.tensor_copy(out=gate[:], in_=unit["v_sum"][:, c - 1 : c])
+            engine = nc.gpsimd if c > 0 else nc.vector
+            engine.tensor_tensor(out=chunk[:], in0=unit["noises"][c][:], in1=chunk[:], op=ALU.mult)
+
+        def phase1_sum(unit, c):
+            v = unit["chunks"][c]
+            nc.vector.scalar_tensor_tensor(
+                out=v[:], in0=v[:], scalar=1.0, in1=unit["means"][c][:],
+                op0=ALU.mult, op1=ALU.add, accum_out=unit["v_sum"][:, c : c + 1],
+            )
+            if c == 0:
+                nc.vector.tensor_scalar_mul(
+                    out=unit["neg_shift"][:], in0=unit["v_sum"][:, 0:1], scalar1=-1.0 / CHUNK
                 )
-                kept["chunks"].append(v)
+            square_sum(v, unit["neg_shift"][:], unit["v_sq"][:, c : c + 1])
 
         def layer_norm_statistics(kept):
             mu = stats.tile([P, 1], F32)
             nc.vector.reduce_sum(out=mu[:], in_=kept["v_sum"][:], axis=AXIS_X)
-            nc.vector.tensor_scalar_mul(out=mu[:], in0=mu[:], scalar1=1.0 / K)
+            nc.gpsimd.tensor_scalar(
+                out=mu[:], in0=mu[:], scalar1=1.0 / K, scalar2=0.0, op0=ALU.mult, op1=ALU.add
+            )
             off = stats.tile([P, 1], F32)
-            nc.vector.tensor_add(out=off[:], in0=mu[:], in1=kept["neg_shift"][:])
-            nc.vector.tensor_mul(out=off[:], in0=off[:], in1=off[:])
+            nc.gpsimd.tensor_tensor(out=off[:], in0=mu[:], in1=kept["neg_shift"][:], op=ALU.add)
+            nc.gpsimd.tensor_tensor(out=off[:], in0=off[:], in1=off[:], op=ALU.mult)
             var = stats.tile([P, 1], F32)
             nc.vector.reduce_sum(out=var[:], in_=kept["v_sq"][:], axis=AXIS_X)
-            nc.vector.scalar_tensor_tensor(
-                out=var[:], in0=var[:], scalar=1.0 / K, in1=off[:], op0=ALU.mult, op1=ALU.subtract
+            nc.gpsimd.tensor_scalar(
+                out=var[:], in0=var[:], scalar1=1.0 / K, scalar2=LN_EPS, op0=ALU.mult, op1=ALU.add
             )
-            nc.vector.tensor_scalar_add(out=var[:], in0=var[:], scalar1=LN_EPS)
             rstd = stats.tile([P, 1], F32)
+            nc.gpsimd.tensor_tensor(out=var[:], in0=var[:], in1=off[:], op=ALU.subtract)
             nc.gpsimd.tensor_tensor(out=rstd[:], in0=var[:], in1=neg_half[:], op=ALU.pow)
             kept["mu"] = mu
             kept["rstd"] = rstd
 
-        def phase2_chunk(kept, c):
-            v = kept["chunks"][c]
-            halves = range(0, CHUNK, BANK_BF16)
-            for first in halves:
-                part = v[:, first : first + BANK_BF16]
-                gain = spread_over_partitions((c * CHUNK + first) // (2 * P), "gain")
+        def phase2_spread(unit, c):
+            unit["gain"] = []
+            unit["bias"] = []
+            for first in range(0, CHUNK, BANK_BF16):
+                unit["gain"].append(spread_over_partitions((c * CHUNK + first) // (2 * P), "gain"))
+            for first in range(0, CHUNK, BANK_BF16):
+                unit["bias"].append(
+                    spread_over_partitions(BIAS_COLUMN + (c * CHUNK + first) // (2 * P), "bias")
+                )
+
+        def phase2_apply(unit, c):
+            v = unit["chunks"][c]
+            for half in range(CHUNK // BANK_BF16):
+                part = v[:, half * BANK_BF16 : (half + 1) * BANK_BF16]
                 nc.vector.scalar_tensor_tensor(
-                    out=part, in0=part, scalar=kept["mu"][:], in1=gain,
+                    out=part, in0=part, scalar=unit["mu"][:], in1=unit["gain"][half],
                     op0=ALU.subtract, op1=ALU.mult,
                 )
-            for first in halves:
-                part = v[:, first : first + BANK_BF16]
-                bias = spread_over_partitions(BIAS_COLUMN + (c * CHUNK + first) // (2 * P), "bias")
+            for half in range(CHUNK // BANK_BF16):
+                part = v[:, half * BANK_BF16 : (half + 1) * BANK_BF16]
                 nc.vector.scalar_tensor_tensor(
-                    out=part, in0=part, scalar=kept["rstd"][:], in1=bias,
+                    out=part, in0=part, scalar=unit["rstd"][:], in1=unit["bias"][half],
                     op0=ALU.mult, op1=ALU.add,
                 )
-            squares = rows.tile([P, CHUNK], BF16, tag="squares")
-            nc.scalar.activation(
-                out=squares[:], in_=v[:], func=ACT.Square, accum_out=kept["u_sq"][:, c : c + 1]
+
+        def phase2_square(unit, c):
+            total = unit["u_sq"][:, c : c + 1]
+            u = unit["chunks"][c]
+            if c < N_CHUNKS:
+                square_sum(u, 0.0, total)
+                return
+            unread = rows.tile([P, CHUNK], BF16, tag="row16", bufs=3)
+            nc.vector.scalar_tensor_tensor(
+                out=unread[:], in0=u[:], scalar=1.0, in1=u[:], op0=ALU.mult, op1=ALU.mult,
+                accum_out=total,
             )
 
         def l2_norm_statistics(kept):
             norm2 = stats.tile([P, 1], F32)
             nc.vector.reduce_sum(out=norm2[:], in_=kept["u_sq"][:], axis=AXIS_X)
-            nc.vector.tensor_scalar_max(out=norm2[:], in0=norm2[:], scalar1=1e-24)
+            nc.gpsimd.tensor_scalar(
+                out=norm2[:], in0=norm2[:], scalar1=1e-24, scalar2=0.0, op0=ALU.max, op1=ALU.add
+            )
             inv_norm = stats.tile([P, 1], F32)
             nc.gpsimd.tensor_tensor(out=inv_norm[:], in0=norm2[:], in1=neg_half[:], op=ALU.pow)
             kept["inv_norm"] = inv_norm
 
-        def phase3_chunk(side, sample, c):
-            kept = held[side][sample]
-            chunk_words = slice(c * WORDS_PER_CHUNK, (c + 1) * WORDS_PER_CHUNK)
-            unit16 = rows.tile([P, CHUNK], BF16, tag="row16")
-            if side == FEATURES and sample == 1:
+        def phase3_round(unit, c, engine):
+            if not inside(c):
+                return
+            unit16 = rows.tile([P, CHUNK], BF16, tag="row16", bufs=3)
+            if engine == nc.scalar:
                 nc.scalar.activation(
-                    out=unit16[:], in_=kept["chunks"][c][:], func=ACT.Copy, scale=kept["inv_norm"][:]
-                )
-            elif side == PROTOTYPES and sample == 0:
-                nc.gpsimd.tensor_scalar(
-                    out=unit16[:], in0=kept["chunks"][c][:], scalar1=kept["inv_norm"][:], scalar2=0.0,
-                    op0=ALU.mult, op1=ALU.add,
+                    out=unit16[:], in_=unit["chunks"][c][:], func=ACT.Copy, scale=unit["inv_norm"][:]
                 )
             else:
-                nc.vector.tensor_scalar_mul(
-                    out=unit16[:], in0=kept["chunks"][c][:], scalar1=kept["inv_norm"][:]
+                engine.tensor_scalar(
+                    out=unit16[:], in0=unit["chunks"][c][:], scalar1=unit["inv_norm"][:],
+                    scalar2=0.0, op0=ALU.mult, op1=ALU.add,
                 )
-            if side == FEATURES:
-                quantise_rows(
-                    unit16, x_codes[sample][:, chunk_words], x_scales[sample][:, chunk_words]
-                )
+            unit["rounded"].append(unit16)
+
+        def phase3_turn(unit, c, copies):
+            if inside(c):
+                unit["grouped"].append(turn_rows(unit["rounded"][c], copies))
+
+        def phase3_quantise(unit, c):
+            if not inside(c):
                 return
-            p_codes = packs.tile([P, WORDS_PER_CHUNK], U32, align_bytes=64, tag="codes")
-            p_scales = packs.tile([P, WORDS_PER_CHUNK], U8, align_bytes=64, tag="scales")
-            quantise_rows(unit16, p_codes[:], p_scales[:])
+            sample = unit["sample"]
+            grouped = unit["grouped"][c]
+            if unit["side"] == FEATURES:
+                chunk_words = slice(c * WORDS_PER_CHUNK, (c + 1) * WORDS_PER_CHUNK)
+                quantise(grouped, x_codes[sample][:, chunk_words], x_scales[sample][:, chunk_words])
+                return
+            p_codes = packs.tile([P, WORDS_PER_CHUNK], U32, align_bytes=64, tag="codes", bufs=2)
+            p_scales = packs.tile([P, WORDS_PER_CHUNK], U8, align_bytes=64, tag="scales", bufs=2)
+            quantise(grouped, p_codes[:], p_scales[:])
             for g in range(PASSES_PER_CHUNK):
                 one = slice(g * P, (g + 1) * P)
                 x_one = slice(c * WORDS_PER_CHUNK + g * P, c * WORDS_PER_CHUNK + (g + 1) * P)
@@ -265,53 +303,204 @@ def tile_probprotoseghead_k_kernel(
                         ),
                     )
 
-        held = []
+        cross_done = []
+        cross = {"count": 0, "loaded": [], "started": [], "turned": [], "age": 0}
+
+        def cross_load():
+            held_tiles = len(cross["loaded"]) + len(cross["started"])
+            if cross["count"] < len(CROSS_ORDER) and held_tiles < 2:
+                side, j = CROSS_ORDER[cross["count"]]
+                cross["loaded"].append(load(units[2 * side]["logvar"], j, "cross_logvar", 2))
+                cross["count"] = cross["count"] + 1
+
+        def cross_piece():
+            if cross["started"]:
+                side, j, std16, made = cross["started"][0]
+                if not made:
+                    nc.scalar.activation(out=std16[:], in_=std16[:], func=ACT.Exp, scale=0.5)
+                    cross["started"].clear()
+                    cross["started"].append((side, j, std16, True))
+                return
+            if not cross["loaded"]:
+                return
+            side, j = CROSS_ORDER[cross["count"] - len(cross["loaded"])]
+            logvar = cross["loaded"][0]
+            cross["loaded"].remove(logvar)
+            total = (xv_parts, pv_parts)[side][:, j : j + 1]
+            std = live_std.get((side, j), None)
+            if std is None:
+                unread = loads.tile([P, CHUNK], BF16, tag="squares", bufs=1)
+                nc.scalar.activation(out=unread[:], in_=logvar[:], func=ACT.Exp, accum_out=total)
+                cross["started"].append((side, j, logvar, False))
+            else:
+                std16 = rows.tile([P, CHUNK], BF16, tag="row16", bufs=3)
+                nc.vector.tensor_copy(out=std16[:], in_=std[:])
+                nc.scalar.activation(out=logvar[:], in_=logvar[:], func=ACT.Exp, accum_out=total)
+                cross["started"].append((side, j, std16, True))
+
+        def cross_turn(copies):
+            if cross["started"] and cross["started"][0][3]:
+                cross_finish(True)
+                side, j, std16, made = cross["started"][0]
+                cross["started"].clear()
+                cross["turned"].append((side, j, turn_rows(std16, copies)))
+                cross["age"] = 0
+
+        def cross_finish(now=False):
+            if not cross["turned"]:
+                return
+            cross["age"] = cross["age"] + 1
+            if cross["age"] < 2 and not now:
+                return
+            side, j, grouped = cross["turned"][0]
+            cross["turned"].clear()
+            if side == FEATURES:
+                codes = packs.tile([P, WORDS_PER_CHUNK], U32, align_bytes=64, tag="cross_codes", bufs=1)
+                scales = packs.tile([P, WORDS_PER_CHUNK], U8, align_bytes=64, tag="cross_scales", bufs=1)
+                quantise(grouped, codes[:], scales[:])
+                cross["x"] = (codes, scales)
+                return
+            codes = packs.tile([P, WORDS_PER_CHUNK], U32, align_bytes=64, tag="codes", bufs=2)
+            scales = packs.tile([P, WORDS_PER_CHUNK], U8, align_bytes=64, tag="scales", bufs=2)
+            quantise(grouped, codes[:], scales[:])
+            xc, xs = cross["x"]
+            for g in range(PASSES_PER_CHUNK):
+                one = slice(g * P, (g + 1) * P)
+                nc.tensor.matmul_mx(
+                    out=cross_sum[:],
+                    lhsT=xc[:, one].bitcast(FP8X4),
+                    lhsT_scale=xs[:, one],
+                    rhs=codes[:, one].bitcast(FP8X4),
+                    rhs_scale=scales[:, one],
+                    start=(len(cross_done) == 0 and g == 0),
+                    stop=(len(cross_done) == N_CHUNKS - 1 and g == PASSES_PER_CHUNK - 1),
+                )
+            cross_done.append(j)
+
+        units = []
         for side in (FEATURES, PROTOTYPES):
-            held.append([])
             for sample in range(SAMPLES):
                 v_sum = stats.tile([P, N_CHUNKS], F32)
                 v_sq = stats.tile([P, N_CHUNKS], F32)
                 u_sq = stats.tile([P, N_CHUNKS], F32)
                 neg_shift = stats.tile([P, 1], F32)
-                held[side].append(
-                    {"v_sum": v_sum, "v_sq": v_sq, "u_sq": u_sq, "neg_shift": neg_shift, "chunks": []}
+                mean_rows, logvar_rows, noise_rows = sides[side]
+                units.append(
+                    {
+                        "side": side, "sample": sample, "mean": mean_rows, "logvar": logvar_rows,
+                        "noise": noise_rows[sample], "v_sum": v_sum, "v_sq": v_sq, "u_sq": u_sq,
+                        "neg_shift": neg_shift, "logvars": [], "noises": [], "means": [], "chunks": [],
+                        "rounded": [], "grouped": [],
+                    }
                 )
+        def inside(c):
+            return 0 <= c < N_CHUNKS
 
-        cross_done = []
+        both = (nc.scalar.copy, nc.scalar.copy)
+        ctx.enter_context(tc.manual_schedule())
 
-        def next_cross_chunk():
-            cross_chunk(len(cross_done))
-            cross_done.append(len(cross_done))
+        def extra(stage, i):
+            cross_turn(both)
+            cross_load()
+            for piece in range(PIECES[stage][i]):
+                cross_piece()
+                cross_load()
 
-        for c in range(N_CHUNKS):
-            phase1_chunk(FEATURES, c)
-        for kept in held[FEATURES]:
-            layer_norm_statistics(kept)
-        for kept in held[FEATURES]:
-            for c in range(N_CHUNKS):
-                phase2_chunk(kept, c)
-                if c % CROSS_EVERY == 1:
-                    next_cross_chunk()
-            l2_norm_statistics(kept)
-        for c in range(N_CHUNKS):
-            for sample in range(SAMPLES):
-                phase3_chunk(FEATURES, sample, c)
-            phase1_chunk(PROTOTYPES, c)
-        for kept in held[PROTOTYPES]:
-            layer_norm_statistics(kept)
-        for c in range(N_CHUNKS):
-            phase2_chunk(held[PROTOTYPES][0], c)
-            if c % CROSS_EVERY == 1:
-                next_cross_chunk()
-        l2_norm_statistics(held[PROTOTYPES][0])
-        for c in range(N_CHUNKS):
-            phase3_chunk(PROTOTYPES, 0, c)
-            phase2_chunk(held[PROTOTYPES][1], c)
-            if c % CROSS_EVERY == 1:
-                next_cross_chunk()
-        l2_norm_statistics(held[PROTOTYPES][1])
-        for c in range(N_CHUNKS):
-            phase3_chunk(PROTOTYPES, 1, c)
+        x0, x1, p0, p1 = units
+        halves = (slice(0, CHUNK // 2), slice(CHUNK // 2, CHUNK))
+        logvar = loads.tile([P, CHUNK], BF16, tag="logvar", bufs=2)
+        noise = loads.tile([P, CHUNK], BF16, tag="noise", bufs=3)
+        x1["logvars"].append(logvar)
+        x0["noises"].append(noise)
+        for half in halves:
+            nc.sync.dma_start(out=logvar[:, half], in_=x_var[:, half])
+            nc.sync.dma_start(out=noise[:, half], in_=eps_x[0][:, half])
+        load_logvar(x1, 1)
+        load_mean(x0, 0)
+        load_noise(x0, 1)
+        std = vpool.tile([P, CHUNK], F32, tag="v1")
+        x1["chunks"].append(std)
+        live_std[(FEATURES, 0)] = std
+        for half in halves:
+            nc.scalar.activation(out=std[:, half], in_=logvar[:, half], func=ACT.Exp, scale=0.5)
+        phase1_std(x1, 1)
+        load_logvar(x1, 2)
+        for first, second, third, s in ((x0, x1, None, 1), (p0, p1, x1, 4)):
+            for i in range(N_CHUNKS + 1):
+                load_logvar(second, i + 3)
+                load_noise(first, i + 2)
+                if third is not None:
+                    phase3_round(third, i + 2, nc.vector)
+                phase1_std(second, i + 2)
+                if inside(i):
+                    phase1_first(first, second, i)
+                if inside(i - 1):
+                    phase1_sum(first, i - 1)
+                load_mean(first, i + 1)
+                if third is not None:
+                    phase3_quantise(third, i)
+                    phase3_turn(third, i + 2, both)
+                cross_finish()
+                extra(s, i)
+            if s == 1:
+                load_gain_and_bias()
+                turn_gain_and_bias()
+            load_noise(second, 0)
+            load_noise(second, 1)
+            load_mean(second, 0)
+            phase1_second(second, 0)
+            layer_norm_statistics(first)
+            phase2_spread(first, 0)
+
+            for i in range(N_CHUNKS):
+                load_noise(second, i + 2)
+                load_mean(second, i + 1)
+                phase1_sum(second, i)
+                if inside(i - 1):
+                    phase2_square(first, i - 1)
+                if inside(i + 1):
+                    phase1_second(second, i + 1)
+                cross_finish()
+                phase2_apply(first, i)
+                phase2_spread(*((first, i + 1) if inside(i + 1) else (second, 0)))
+                extra(s + 1, i)
+            phase2_square(first, N_CHUNKS - 1)
+            layer_norm_statistics(second)
+            l2_norm_statistics(first)
+
+            phase3_round(first, 0, nc.vector)
+            for i in range(N_CHUNKS + 1):
+                phase3_round(first, i + 1, nc.gpsimd)
+                phase3_turn(first, i, both)
+                if inside(i):
+                    phase2_apply(second, i)
+                if inside(i + 1):
+                    phase2_spread(second, i + 1)
+                phase3_quantise(first, i - 1)
+                cross_finish()
+                if inside(i):
+                    phase2_square(second, i)
+                extra(s + 2, i)
+            l2_norm_statistics(second)
+            if s == 1:
+                load_logvar(p1, 0)
+                load_logvar(p1, 1)
+                load_noise(p0, 0)
+                load_mean(p0, 0)
+                load_noise(p0, 1)
+                for c in range(2):
+                    phase3_round(x1, c, nc.vector)
+                    phase1_std(p1, c)
+                    phase3_turn(x1, c, both)
+                load_logvar(p1, 2)
+
+        for i in range(N_CHUNKS + 2):
+            phase3_round(p1, i, nc.gpsimd if i % 3 == 2 else nc.vector)
+            phase3_quantise(p1, i - 2)
+            if i in (1, 4):
+                cross_finish(True)
+            phase3_turn(p1, i, both)
+            extra(7, i)
 
         xv_term = const.tile([P, 1], F32)
         nc.vector.reduce_sum(out=xv_term[:], in_=xv_parts[:], axis=AXIS_X)
@@ -321,7 +510,10 @@ def tile_probprotoseghead_k_kernel(
         pv_sum = const.tile([P, 1], F32)
         nc.vector.reduce_sum(out=pv_sum[:], in_=pv_parts[:], axis=AXIS_X)
         pv_repeated = const.tile([P, P], F32)
-        nc.vector.tensor_scalar_mul(out=pv_repeated[:], in0=ones[:], scalar1=pv_sum[:])
+        nc.vector.tensor_scalar(
+            out=pv_repeated[:], in0=ident[:], scalar1=0.0, scalar2=pv_sum[:],
+            op0=ALU.mult, op1=ALU.add,
+        )
         pv_bank = flipped.tile([P, 2, 2, P], F32, tag="bank")
         pv_along = pv_bank[:, 0, 0, :]
         nc.tensor.transpose(pv_along, pv_repeated[:], ident[:])

@@ -109,8 +109,18 @@ def tile_probprotoseghead_k_kernel(
                 )
             return grouped
 
+        gate_word = const.tile([P, 1], U32)
+        quantised = []
+
         def quantise(grouped, codes, scales):
             nc.vector.quantize_mx(out=codes.bitcast(FP8X4), scales=scales, in_=grouped[:])
+            quantised.clear()
+            quantised.append(codes[:, 0:1])
+
+        def gate_on_quantise():
+            if quantised:
+                nc.gpsimd.tensor_copy(out=gate_word[:], in_=quantised[0])
+                quantised.clear()
 
         wb_rows = const.tile([P, 2 * P], BF16)
         wb_cols = const.tile([P, P], F32)
@@ -458,9 +468,10 @@ def tile_probprotoseghead_k_kernel(
                 phase1_sum(second, i)
                 if inside(i - 1):
                     phase2_square(first, i - 1)
-                if inside(i + 1):
-                    phase1_second(second, i + 1)
                 cross_finish()
+                if inside(i + 1):
+                    gate_on_quantise()
+                    phase1_second(second, i + 1)
                 phase2_apply(first, i)
                 phase2_spread(*((first, i + 1) if inside(i + 1) else (second, 0)))
                 extra(s + 1, i)
@@ -469,8 +480,8 @@ def tile_probprotoseghead_k_kernel(
             l2_norm_statistics(first)
 
             phase3_round(first, 0, nc.vector)
+            phase3_round(first, 1, nc.gpsimd)
             for i in range(N_CHUNKS + 1):
-                phase3_round(first, i + 1, nc.gpsimd)
                 phase3_turn(first, i, both)
                 if inside(i):
                     phase2_apply(second, i)
@@ -478,6 +489,8 @@ def tile_probprotoseghead_k_kernel(
                     phase2_spread(second, i + 1)
                 phase3_quantise(first, i - 1)
                 cross_finish()
+                gate_on_quantise()
+                phase3_round(first, i + 2, nc.gpsimd)
                 if inside(i):
                     phase2_square(second, i)
                 extra(s + 2, i)
@@ -495,7 +508,7 @@ def tile_probprotoseghead_k_kernel(
                 load_logvar(p1, 2)
 
         for i in range(N_CHUNKS + 2):
-            phase3_round(p1, i, nc.gpsimd if i % 3 == 2 else nc.vector)
+            phase3_round(p1, i, nc.vector)
             phase3_quantise(p1, i - 2)
             if i in (1, 4):
                 cross_finish(True)

@@ -25,6 +25,7 @@ BIAS_COLUMN = K // (2 * P)
 SAMPLES = 2
 FEATURES, PROTOTYPES = 0, 1
 CROSS_ORDER = [(side, j) for j in (0, 1, 7, 6, 2, 3, 4, 5) for side in (0, 1)]
+VECTOR_SHARE = 128
 PIECES = {
     1: (0, 1, 1, 1, 1, 0, 0, 0, 0),
     2: (1, 1, 1, 1, 1, 1, 0, 0),
@@ -176,13 +177,21 @@ def tile_probprotoseghead_k_kernel(
                 )
             unit["chunks"].append(chunk)
 
-        def phase1_second(unit, c):
+        def phase1_second_start(unit, c):
             chunk = unit["chunks"][c]
             live_std[(unit["side"], c)] = None
-            if c > 0:
-                nc.gpsimd.tensor_copy(out=gate[:], in_=unit["v_sum"][:, c - 1 : c])
-            engine = nc.gpsimd if c > 0 else nc.vector
-            engine.tensor_tensor(out=chunk[:], in0=unit["noises"][c][:], in1=chunk[:], op=ALU.mult)
+            early = slice(0, VECTOR_SHARE if c > 0 else CHUNK)
+            nc.vector.tensor_mul(
+                out=chunk[:, early], in0=unit["noises"][c][:, early], in1=chunk[:, early]
+            )
+
+        def phase1_second(unit, c):
+            chunk = unit["chunks"][c]
+            nc.gpsimd.tensor_copy(out=gate[:], in_=unit["v_sum"][:, c - 1 : c])
+            late = slice(VECTOR_SHARE, CHUNK)
+            nc.gpsimd.tensor_tensor(
+                out=chunk[:, late], in0=unit["noises"][c][:, late], in1=chunk[:, late], op=ALU.mult
+            )
 
         def phase1_sum(unit, c):
             v = unit["chunks"][c]
@@ -348,9 +357,10 @@ def tile_probprotoseghead_k_kernel(
                 nc.scalar.activation(out=logvar[:], in_=logvar[:], func=ACT.Exp, accum_out=total)
                 cross["started"].append((side, j, std16, True))
 
-        def cross_turn(copies):
+        def cross_turn(copies, room):
             if cross["started"] and cross["started"][0][3]:
-                cross_finish(True)
+                if len(cross["turned"]) >= room:
+                    cross_finish(True)
                 side, j, std16, made = cross["started"][0]
                 cross["started"].clear()
                 cross["turned"].append((side, j, turn_rows(std16, copies)))
@@ -363,7 +373,7 @@ def tile_probprotoseghead_k_kernel(
             if cross["age"] < 2 and not now:
                 return
             side, j, grouped = cross["turned"][0]
-            cross["turned"].clear()
+            cross["turned"].remove(cross["turned"][0])
             if side == FEATURES:
                 codes = packs.tile([P, WORDS_PER_CHUNK], U32, align_bytes=64, tag="cross_codes", bufs=1)
                 scales = packs.tile([P, WORDS_PER_CHUNK], U8, align_bytes=64, tag="cross_scales", bufs=1)
@@ -410,7 +420,7 @@ def tile_probprotoseghead_k_kernel(
         ctx.enter_context(tc.manual_schedule())
 
         def extra(stage, i):
-            cross_turn(both)
+            cross_turn(both, 2 if stage in (1, 2, 5) else 1)
             cross_load()
             for piece in range(PIECES[stage][i]):
                 cross_piece()
@@ -458,7 +468,7 @@ def tile_probprotoseghead_k_kernel(
             load_noise(second, 0)
             load_noise(second, 1)
             load_mean(second, 0)
-            phase1_second(second, 0)
+            phase1_second_start(second, 0)
             layer_norm_statistics(first)
             phase2_spread(first, 0)
 
@@ -468,6 +478,8 @@ def tile_probprotoseghead_k_kernel(
                 phase1_sum(second, i)
                 if inside(i - 1):
                     phase2_square(first, i - 1)
+                if inside(i + 1):
+                    phase1_second_start(second, i + 1)
                 cross_finish()
                 if inside(i + 1):
                     gate_on_quantise()
@@ -477,42 +489,44 @@ def tile_probprotoseghead_k_kernel(
                 extra(s + 1, i)
             phase2_square(first, N_CHUNKS - 1)
             layer_norm_statistics(second)
-            l2_norm_statistics(first)
 
-            phase3_round(first, 0, nc.vector)
-            phase3_round(first, 1, nc.gpsimd)
-            for i in range(N_CHUNKS + 1):
-                phase3_turn(first, i, both)
-                if inside(i):
-                    phase2_apply(second, i)
+            for i in range(N_CHUNKS):
+                phase2_apply(second, i)
                 if inside(i + 1):
                     phase2_spread(second, i + 1)
-                phase3_quantise(first, i - 1)
+                if i == 0:
+                    l2_norm_statistics(first)
+                phase3_turn(first, i - 1, both)
+                phase3_quantise(first, i - 2)
                 cross_finish()
                 gate_on_quantise()
-                phase3_round(first, i + 2, nc.gpsimd)
-                if inside(i):
-                    phase2_square(second, i)
+                phase3_round(first, i, nc.gpsimd)
+                phase2_square(second, i)
                 extra(s + 2, i)
-            l2_norm_statistics(second)
+            phase3_turn(first, N_CHUNKS - 1, both)
+            phase3_quantise(first, N_CHUNKS - 2)
             if s == 1:
                 load_logvar(p1, 0)
                 load_logvar(p1, 1)
                 load_noise(p0, 0)
                 load_mean(p0, 0)
                 load_noise(p0, 1)
+            l2_norm_statistics(second)
+            phase3_round(second, 0, nc.vector)
+            phase3_round(second, 1, nc.vector)
+            phase3_quantise(first, N_CHUNKS - 1)
+            if s == 1:
                 for c in range(2):
-                    phase3_round(x1, c, nc.vector)
                     phase1_std(p1, c)
                     phase3_turn(x1, c, both)
                 load_logvar(p1, 2)
 
         for i in range(N_CHUNKS + 2):
-            phase3_round(p1, i, nc.vector)
-            phase3_quantise(p1, i - 2)
+            phase3_turn(p1, i, both)
+            phase3_round(p1, i + 2, nc.vector)
+            phase3_quantise(p1, i - 1)
             if i in (1, 4):
                 cross_finish(True)
-            phase3_turn(p1, i, both)
             extra(7, i)
 
         xv_term = const.tile([P, 1], F32)

@@ -24,16 +24,16 @@ BANK_BF16 = 2 * BANK_WORDS
 BIAS_COLUMN = K // (2 * P)
 SAMPLES = 2
 FEATURES, PROTOTYPES = 0, 1
-CROSS_ORDER = [(side, j) for j in (0, 1, 7, 6, 2, 3, 4, 5) for side in (0, 1)]
+CROSS_ORDER = [(side, j) for j in (0, 7, 6, 1, 5, 4, 2, 3) for side in (0, 1)]
 VECTOR_SHARE = 128
 PIECES = {
-    1: (0, 1, 1, 1, 1, 0, 0, 0, 0),
-    2: (1, 1, 1, 1, 1, 1, 0, 0),
+    1: (0, 1, 1, 0, 0, 0, 0, 0, 0),
+    2: (1, 1, 1, 1, 1, 1, 1, 0),
     3: (1, 1, 1, 1, 1, 1, 0, 0, 0),
-    4: (0, 0, 1, 1, 0, 0, 0, 0, 0),
-    5: (1, 1, 1, 1, 1, 1, 0, 0),
+    4: (0, 1, 1, 1, 0, 0, 0, 0, 0),
+    5: (1, 1, 1, 1, 1, 1, 1, 0),
     6: (1, 1, 1, 1, 1, 1, 0, 0, 0),
-    7: (1, 1, 1, 1, 1, 1, 0, 0, 0, 0),
+    7: (1, 1, 1, 0, 0, 0, 0, 0, 0, 0),
 }
 LN_EPS = 1e-5
 LAMDA = 1.0 / (K // 4)
@@ -323,7 +323,7 @@ def tile_probprotoseghead_k_kernel(
                     )
 
         cross_done = []
-        cross = {"count": 0, "loaded": [], "started": [], "turned": [], "age": 0}
+        cross = {"count": 0, "loaded": [], "started": [], "turned": []}
 
         def cross_load():
             held_tiles = len(cross["loaded"]) + len(cross["started"])
@@ -363,17 +363,20 @@ def tile_probprotoseghead_k_kernel(
                     cross_finish(True)
                 side, j, std16, made = cross["started"][0]
                 cross["started"].clear()
-                cross["turned"].append((side, j, turn_rows(std16, copies)))
-                cross["age"] = 0
+                cross["turned"].append({"half": (side, j), "grouped": turn_rows(std16, copies), "age": 0})
 
         def cross_finish(now=False):
             if not cross["turned"]:
                 return
-            cross["age"] = cross["age"] + 1
-            if cross["age"] < 2 and not now:
-                return
-            side, j, grouped = cross["turned"][0]
-            cross["turned"].remove(cross["turned"][0])
+            if not now:
+                for turned in cross["turned"]:
+                    turned["age"] = turned["age"] + 1
+                if cross["turned"][0]["age"] < 2:
+                    return
+            oldest = cross["turned"][0]
+            cross["turned"].remove(oldest)
+            side, j = oldest["half"]
+            grouped = oldest["grouped"]
             if side == FEATURES:
                 codes = packs.tile([P, WORDS_PER_CHUNK], U32, align_bytes=64, tag="cross_codes", bufs=1)
                 scales = packs.tile([P, WORDS_PER_CHUNK], U8, align_bytes=64, tag="cross_scales", bufs=1)
@@ -420,7 +423,7 @@ def tile_probprotoseghead_k_kernel(
         ctx.enter_context(tc.manual_schedule())
 
         def extra(stage, i):
-            cross_turn(both, 2 if stage in (1, 2, 5) else 1)
+            cross_turn(both, 2 if stage == 1 or (stage in (2, 5) and i < 5) else 1)
             cross_load()
             for piece in range(PIECES[stage][i]):
                 cross_piece()
@@ -505,6 +508,7 @@ def tile_probprotoseghead_k_kernel(
                 extra(s + 2, i)
             phase3_turn(first, N_CHUNKS - 1, both)
             phase3_quantise(first, N_CHUNKS - 2)
+            cross_finish(True)
             if s == 1:
                 load_logvar(p1, 0)
                 load_logvar(p1, 1)
@@ -521,6 +525,34 @@ def tile_probprotoseghead_k_kernel(
                     phase3_turn(x1, c, both)
                 load_logvar(p1, 2)
 
+        xv_term = const.tile([P, 1], F32)
+        pv_sum = const.tile([P, 1], F32)
+        pv_repeated = const.tile([P, P], F32)
+        result = const.tile([P, P], F32)
+
+        def all_but_the_samples():
+            nc.vector.reduce_sum(out=xv_term[:], in_=xv_parts[:], axis=AXIS_X)
+            nc.vector.tensor_scalar(
+                out=xv_term[:], in0=xv_term[:], scalar1=-LAMDA, scalar2=-2.0, op0=ALU.mult, op1=ALU.add
+            )
+            nc.vector.reduce_sum(out=pv_sum[:], in_=pv_parts[:], axis=AXIS_X)
+            nc.vector.tensor_scalar(
+                out=pv_repeated[:], in0=ident[:], scalar1=0.0, scalar2=pv_sum[:],
+                op0=ALU.mult, op1=ALU.add,
+            )
+            pv_bank = spread.tile([P, BANK_WORDS], F32, tag="gain")
+            pv_along = pv_bank[:, 0:P]
+            nc.tensor.transpose(pv_along, pv_repeated[:], ident[:])
+
+            nc.vector.tensor_scalar(
+                out=result[:], in0=cross_sum[:], scalar1=2.0 * LAMDA, scalar2=xv_term[:],
+                op0=ALU.mult, op1=ALU.add,
+            )
+            nc.vector.scalar_tensor_tensor(
+                out=result[:], in0=pv_along, scalar=-LAMDA, in1=result[:],
+                op0=ALU.mult, op1=ALU.add,
+            )
+
         for i in range(N_CHUNKS + 2):
             phase3_turn(p1, i, both)
             phase3_round(p1, i + 2, nc.vector)
@@ -528,32 +560,9 @@ def tile_probprotoseghead_k_kernel(
             if i in (1, 4):
                 cross_finish(True)
             extra(7, i)
+            if i == N_CHUNKS - 2:
+                all_but_the_samples()
 
-        xv_term = const.tile([P, 1], F32)
-        nc.vector.reduce_sum(out=xv_term[:], in_=xv_parts[:], axis=AXIS_X)
-        nc.vector.tensor_scalar(
-            out=xv_term[:], in0=xv_term[:], scalar1=-LAMDA, scalar2=-2.0, op0=ALU.mult, op1=ALU.add
-        )
-        pv_sum = const.tile([P, 1], F32)
-        nc.vector.reduce_sum(out=pv_sum[:], in_=pv_parts[:], axis=AXIS_X)
-        pv_repeated = const.tile([P, P], F32)
-        nc.vector.tensor_scalar(
-            out=pv_repeated[:], in0=ident[:], scalar1=0.0, scalar2=pv_sum[:],
-            op0=ALU.mult, op1=ALU.add,
-        )
-        pv_bank = flipped.tile([P, 2, 2, P], F32, tag="bank")
-        pv_along = pv_bank[:, 0, 0, :]
-        nc.tensor.transpose(pv_along, pv_repeated[:], ident[:])
-
-        result = const.tile([P, P], F32)
-        nc.vector.tensor_scalar(
-            out=result[:], in0=cross_sum[:], scalar1=2.0 * LAMDA, scalar2=xv_term[:],
-            op0=ALU.mult, op1=ALU.add,
-        )
-        nc.vector.scalar_tensor_tensor(
-            out=result[:], in0=pv_along, scalar=-LAMDA, in1=result[:],
-            op0=ALU.mult, op1=ALU.add,
-        )
         nc.vector.scalar_tensor_tensor(
             out=result[:], in0=sim_sum[:], scalar=0.5, in1=result[:], op0=ALU.mult, op1=ALU.add
         )

@@ -27,13 +27,13 @@ FEATURES, PROTOTYPES = 0, 1
 CROSS_ORDER = [(side, j) for j in (0, 7, 6, 1, 5, 4, 2, 3) for side in (0, 1)]
 VECTOR_SHARE = 128
 PIECES = {
-    1: (0, 1, 1, 0, 0, 0, 0, 0, 0),
+    1: (0, 0, 1, 1, 0, 0, 0, 0, 0),
     2: (1, 1, 1, 1, 1, 1, 1, 0),
     3: (1, 1, 1, 1, 1, 1, 0, 0, 0),
-    4: (0, 1, 1, 1, 0, 0, 0, 0, 0),
+    4: (0, 0, 1, 1, 0, 0, 0, 0, 0),
     5: (1, 1, 1, 1, 1, 1, 1, 0),
     6: (1, 1, 1, 1, 1, 1, 0, 0, 0),
-    7: (1, 1, 1, 0, 0, 0, 0, 0, 0, 0),
+    7: (1, 1, 1, 1, 0, 0, 0, 0, 0, 0),
 }
 LN_EPS = 1e-5
 LAMDA = 1.0 / (K // 4)
@@ -141,8 +141,16 @@ def tile_probprotoseghead_k_kernel(
             return tile
 
         def load_logvar(unit, c):
-            if inside(c):
-                unit["logvars"].append(load(unit["logvar"], c, "logvar", 2))
+            if not inside(c):
+                return
+            if unit["side"] == FEATURES and c % 2 == 1:
+                logvar = rows.tile([P, CHUNK], BF16, tag="row16", bufs=3)
+                nc.sync.dma_start(
+                    out=logvar[:], in_=unit["logvar"][:, c * CHUNK : (c + 1) * CHUNK]
+                )
+            else:
+                logvar = load(unit["logvar"], c, "logvar", 2)
+            unit["logvars"].append(logvar)
 
         def load_noise(unit, c):
             if inside(c):
@@ -155,7 +163,7 @@ def tile_probprotoseghead_k_kernel(
         def square_sum(values, bias, total):
             squares = loads.tile([P, CHUNK], BF16, tag="squares", bufs=1)
             nc.scalar.activation(
-                out=squares[:], in_=values[:], func=ACT.Square, bias=bias, accum_out=total
+                out=squares[:, 0 : values.shape[1]], in_=values, func=ACT.Square, bias=bias, accum_out=total
             )
 
         gate = const.tile([P, 1], F32)
@@ -187,7 +195,10 @@ def tile_probprotoseghead_k_kernel(
 
         def phase1_second(unit, c):
             chunk = unit["chunks"][c]
-            nc.gpsimd.tensor_copy(out=gate[:], in_=unit["v_sum"][:, c - 1 : c])
+            if quantised:
+                gate_on_quantise()
+            else:
+                nc.gpsimd.tensor_copy(out=gate[:], in_=unit["v_sum"][:, c - 1 : c])
             late = slice(VECTOR_SHARE, CHUNK)
             nc.gpsimd.tensor_tensor(
                 out=chunk[:, late], in0=unit["noises"][c][:, late], in1=chunk[:, late], op=ALU.mult
@@ -203,9 +214,9 @@ def tile_probprotoseghead_k_kernel(
                 nc.vector.tensor_scalar_mul(
                     out=unit["neg_shift"][:], in0=unit["v_sum"][:, 0:1], scalar1=-1.0 / CHUNK
                 )
-            square_sum(v, unit["neg_shift"][:], unit["v_sq"][:, c : c + 1])
+            square_sum(v[:], unit["neg_shift"][:], unit["v_sq"][:, c : c + 1])
 
-        def layer_norm_statistics(kept):
+        def mean_statistics(kept):
             mu = stats.tile([P, 1], F32)
             nc.vector.reduce_sum(out=mu[:], in_=kept["v_sum"][:], axis=AXIS_X)
             nc.gpsimd.tensor_scalar(
@@ -214,15 +225,21 @@ def tile_probprotoseghead_k_kernel(
             off = stats.tile([P, 1], F32)
             nc.gpsimd.tensor_tensor(out=off[:], in0=mu[:], in1=kept["neg_shift"][:], op=ALU.add)
             nc.gpsimd.tensor_tensor(out=off[:], in0=off[:], in1=off[:], op=ALU.mult)
+            nc.gpsimd.tensor_scalar(
+                out=off[:], in0=off[:], scalar1=1.0, scalar2=-LN_EPS, op0=ALU.mult, op1=ALU.add
+            )
+            kept["mu"] = mu
+            kept["off"] = off
+
+        def variance_statistics(kept):
             var = stats.tile([P, 1], F32)
             nc.vector.reduce_sum(out=var[:], in_=kept["v_sq"][:], axis=AXIS_X)
-            nc.gpsimd.tensor_scalar(
-                out=var[:], in0=var[:], scalar1=1.0 / K, scalar2=LN_EPS, op0=ALU.mult, op1=ALU.add
+            nc.vector.scalar_tensor_tensor(
+                out=var[:], in0=var[:], scalar=1.0 / K, in1=kept["off"][:],
+                op0=ALU.mult, op1=ALU.subtract,
             )
             rstd = stats.tile([P, 1], F32)
-            nc.gpsimd.tensor_tensor(out=var[:], in0=var[:], in1=off[:], op=ALU.subtract)
             nc.gpsimd.tensor_tensor(out=rstd[:], in0=var[:], in1=neg_half[:], op=ALU.pow)
-            kept["mu"] = mu
             kept["rstd"] = rstd
 
         def phase2_spread(unit, c):
@@ -251,15 +268,17 @@ def tile_probprotoseghead_k_kernel(
                 )
 
         def phase2_square(unit, c):
-            total = unit["u_sq"][:, c : c + 1]
             u = unit["chunks"][c]
-            if c < N_CHUNKS:
-                square_sum(u, 0.0, total)
+            total = unit["u_sq"][:, c : c + 1]
+            if unit["sample"] == 0 or c < N_CHUNKS - 1:
+                square_sum(u[:], 0.0, total)
                 return
-            unread = rows.tile([P, CHUNK], BF16, tag="row16", bufs=3)
+            half = CHUNK // 2
+            square_sum(u[:, 0:half], 0.0, total)
+            unread = rows.tile([P, half], BF16, tag="row16", bufs=3)
             nc.vector.scalar_tensor_tensor(
-                out=unread[:], in0=u[:], scalar=1.0, in1=u[:], op0=ALU.mult, op1=ALU.mult,
-                accum_out=total,
+                out=unread[:], in0=u[:, half:CHUNK], scalar=1.0, in1=u[:, half:CHUNK],
+                op0=ALU.mult, op1=ALU.mult, accum_out=unit["u_sq"][:, N_CHUNKS : N_CHUNKS + 1],
             )
 
         def l2_norm_statistics(kept):
@@ -405,7 +424,7 @@ def tile_probprotoseghead_k_kernel(
             for sample in range(SAMPLES):
                 v_sum = stats.tile([P, N_CHUNKS], F32)
                 v_sq = stats.tile([P, N_CHUNKS], F32)
-                u_sq = stats.tile([P, N_CHUNKS], F32)
+                u_sq = stats.tile([P, N_CHUNKS + sample], F32)
                 neg_shift = stats.tile([P, 1], F32)
                 mean_rows, logvar_rows, noise_rows = sides[side]
                 units.append(
@@ -424,10 +443,8 @@ def tile_probprotoseghead_k_kernel(
 
         def extra(stage, i):
             cross_turn(both, 2 if stage == 1 or (stage in (2, 5) and i < 5) else 1)
-            cross_load()
             for piece in range(PIECES[stage][i]):
                 cross_piece()
-                cross_load()
 
         x0, x1, p0, p1 = units
         halves = (slice(0, CHUNK // 2), slice(CHUNK // 2, CHUNK))
@@ -446,12 +463,14 @@ def tile_probprotoseghead_k_kernel(
         live_std[(FEATURES, 0)] = std
         for half in halves:
             nc.scalar.activation(out=std[:, half], in_=logvar[:, half], func=ACT.Exp, scale=0.5)
-        phase1_std(x1, 1)
         load_logvar(x1, 2)
+        load_logvar(x1, 3)
+        phase1_std(x1, 1)
         for first, second, third, s in ((x0, x1, None, 1), (p0, p1, x1, 4)):
             for i in range(N_CHUNKS + 1):
-                load_logvar(second, i + 3)
+                load_logvar(second, i + (4 if third is None else 3))
                 load_noise(first, i + 2)
+                cross_load()
                 if third is not None:
                     phase3_round(third, i + 2, nc.vector)
                 phase1_std(second, i + 2)
@@ -471,29 +490,34 @@ def tile_probprotoseghead_k_kernel(
             load_noise(second, 0)
             load_noise(second, 1)
             load_mean(second, 0)
+            mean_statistics(first)
             phase1_second_start(second, 0)
-            layer_norm_statistics(first)
+            variance_statistics(first)
             phase2_spread(first, 0)
 
             for i in range(N_CHUNKS):
                 load_noise(second, i + 2)
                 load_mean(second, i + 1)
-                phase1_sum(second, i)
-                if inside(i - 1):
-                    phase2_square(first, i - 1)
                 if inside(i + 1):
                     phase1_second_start(second, i + 1)
+                quantised.clear()
+                phase1_sum(second, i)
+                cross_load()
+                if inside(i - 1):
+                    phase2_square(first, i - 1)
                 cross_finish()
                 if inside(i + 1):
-                    gate_on_quantise()
                     phase1_second(second, i + 1)
+                else:
+                    mean_statistics(second)
                 phase2_apply(first, i)
                 phase2_spread(*((first, i + 1) if inside(i + 1) else (second, 0)))
                 extra(s + 1, i)
             phase2_square(first, N_CHUNKS - 1)
-            layer_norm_statistics(second)
+            variance_statistics(second)
 
             for i in range(N_CHUNKS):
+                cross_load()
                 phase2_apply(second, i)
                 if inside(i + 1):
                     phase2_spread(second, i + 1)
@@ -554,6 +578,7 @@ def tile_probprotoseghead_k_kernel(
             )
 
         for i in range(N_CHUNKS + 2):
+            cross_load()
             phase3_turn(p1, i, both)
             phase3_round(p1, i + 2, nc.vector)
             phase3_quantise(p1, i - 1)

from contextlib import ExitStack

import concourse.mybir as mybir
from concourse.masks import make_identity

F32 = mybir.dt.float32
BF16 = mybir.dt.bfloat16
U32 = mybir.dt.uint32
U8 = mybir.dt.uint8
FP8X4 = mybir.dt.float8_e4m3fn_x4
ALU = mybir.AluOpType
ACT = mybir.ActivationFunctionType
AXIS_X = mybir.AxisListType.X

P = 128
K = 16384
CHUNK = 2048
N_CHUNKS = K // CHUNK
K_PASS = 512
PASSES_PER_CHUNK = CHUNK // K_PASS
WORDS_PER_CHUNK = PASSES_PER_CHUNK * P
BANK_WORDS = 512
BANK_BF16 = 2 * BANK_WORDS
BIAS_COLUMN = K // (2 * P)
SAMPLES = 2
FEATURES, PROTOTYPES = 0, 1
CROSS_ORDER = [(side, j) for j in (0, 7, 6, 1, 5, 4, 2, 3) for side in (0, 1)]
VECTOR_SHARE = 128
PIECES = {
    1: (0, 0, 1, 1, 0, 0, 0, 0, 0),
    2: (1, 1, 1, 1, 1, 1, 1, 0),
    3: (1, 1, 1, 1, 1, 1, 0, 0, 0),
    4: (0, 0, 1, 1, 0, 0, 0, 0, 0),
    5: (1, 1, 1, 1, 1, 1, 1, 0),
    6: (1, 1, 1, 1, 1, 1, 0, 0, 0),
    7: (1, 1, 1, 1, 0, 0, 0, 0, 0, 0),
}
LN_EPS = 1e-5
LAMDA = 1.0 / (K // 4)

FLOPS = 2 * (SAMPLES * P) * (SAMPLES * P) * K + 2 * P * P * K


def tile_probprotoseghead_k_kernel(
    tc, x, x_var, prototypes, proto_var, eps_x, eps_p, ln_w, ln_b, out
):
    nc = tc.nc
    proto_rows = prototypes.rearrange("c m k -> (c m) k")
    proto_var_rows = proto_var.rearrange("c m k -> (c m) k")
    sides = [
        (x, x_var, [eps_x[0], eps_x[1]]),
        (
            proto_rows,
            proto_var_rows,
            [eps_p[0].rearrange("c m k -> (c m) k"), eps_p[1].rearrange("c m k -> (c m) k")],
        ),
    ]

    with ExitStack() as ctx:
        const = ctx.enter_context(tc.tile_pool(name="const", bufs=1))
        vpool = ctx.enter_context(tc.tile_pool(name="vpool", bufs=N_CHUNKS))
        loads = ctx.enter_context(tc.tile_pool(name="loads", bufs=3))
        rows = ctx.enter_context(tc.tile_pool(name="rows", bufs=2))
        packs = ctx.enter_context(tc.tile_pool(name="packs", bufs=2))
        stats = ctx.enter_context(tc.tile_pool(name="stats", bufs=2 * SAMPLES))
        flipped = ctx.enter_context(tc.psum_pool(name="flipped", bufs=2))
        spread = ctx.enter_context(tc.psum_pool(name="spread", bufs=2))
        sums = ctx.enter_context(tc.psum_pool(name="sums", bufs=1))

        ident = const.tile([P, P], F32)
        make_identity(nc, ident[:])
        neg_half = const.tile([P, 1], F32)
        nc.vector.memset(neg_half[:], -0.5)

        x_codes0 = const.tile([P, N_CHUNKS * WORDS_PER_CHUNK], U32, align_bytes=64)
        x_codes1 = const.tile([P, N_CHUNKS * WORDS_PER_CHUNK], U32, align_bytes=64)
        x_planes = const.tile([P, N_CHUNKS * WORDS_PER_CHUNK], U8, align_bytes=64)
        x_codes = [x_codes0, x_codes1]
        x_scales = [x_planes[0:P, :], x_planes[4:P, :]]

        sim_sum = sums.tile([P, P], F32)
        cross_sum = sums.tile([P, P], F32)
        xv_parts = const.tile([P, N_CHUNKS], F32)
        pv_parts = const.tile([P, N_CHUNKS], F32)

        def spread_over_partitions(first_column, tag):
            bank = spread.tile([P, BANK_WORDS], F32, tag=tag)
            for i in range(BANK_WORDS // P):
                j = first_column + i
                nc.tensor.transpose(
                    bank[:, i * P : (i + 1) * P], wb_cols[:, j : j + 1].to_broadcast([P, P]), ident[:]
                )
            return bank[:].bitcast(BF16)

        def turn_rows(row16, copies):
            words = row16[:].bitcast(F32).rearrange(
                "p (g u q) -> p g u q", g=PASSES_PER_CHUNK, u=2
            )
            grouped = packs.tile([P, CHUNK], BF16, tag="grouped", bufs=3, align_bytes=64)
            grouped_words = grouped[:].bitcast(F32).rearrange(
                "p (h g n u) -> p h g n u", h=PASSES_PER_CHUNK // 2, g=2, u=2
            )
            for h in range(PASSES_PER_CHUNK // 2):
                bank = flipped.tile([P, 2, 2, P], F32)
                for g in range(2):
                    for u in range(2):
                        nc.tensor.transpose(bank[:, g, u, :], words[:, 2 * h + g, u, :], ident[:])
                copies[h](
                    out=grouped_words[:, h], in_=bank[:].rearrange("p g u n -> p g n u")
                )
            return grouped

        gate_word = const.tile([P, 1], U32)
        quantised = []

        def quantise(grouped, codes, scales):
            nc.vector.quantize_mx(out=codes.bitcast(FP8X4), scales=scales, in_=grouped[:])
            quantised.clear()
            quantised.append(codes[:, 0:1])

        def gate_on_quantise():
            if quantised:
                nc.gpsimd.tensor_copy(out=gate_word[:], in_=quantised[0])
                quantised.clear()

        wb_rows = const.tile([P, 2 * P], BF16)
        wb_cols = const.tile([P, P], F32)

        def load_gain_and_bias():
            nc.sync.dma_start(out=wb_rows[0:BIAS_COLUMN, :], in_=ln_w.rearrange("(j c) -> j c", c=2 * P))
            nc.sync.dma_start(out=wb_rows[BIAS_COLUMN:P, :], in_=ln_b.rearrange("(j c) -> j c", c=2 * P))

        def turn_gain_and_bias():
            turned = spread.tile([P, BANK_WORDS], F32, tag="gain")
            nc.tensor.transpose(turned[:, 0:P], wb_rows[:].bitcast(F32), ident[:])
            nc.vector.tensor_copy(out=wb_cols[:], in_=turned[:, 0:P])

        def load(rows_in_hbm, c, tag, bufs):
            tile = loads.tile([P, CHUNK], BF16, tag=tag, bufs=bufs)
            nc.sync.dma_start(out=tile[:], in_=rows_in_hbm[:, c * CHUNK : (c + 1) * CHUNK])
            return tile

        def load_logvar(unit, c):
            if not inside(c):
                return
            if unit["side"] == FEATURES and c % 2 == 1:
                logvar = rows.tile([P, CHUNK], BF16, tag="row16", bufs=3)
                nc.sync.dma_start(
                    out=logvar[:], in_=unit["logvar"][:, c * CHUNK : (c + 1) * CHUNK]
                )
            else:
                logvar = load(unit["logvar"], c, "logvar", 2)
            unit["logvars"].append(logvar)

        def load_noise(unit, c):
            if inside(c):
                unit["noises"].append(load(unit["noise"], c, "noise", 3))

        def load_mean(unit, c):
            if inside(c):
                unit["means"].append(load(unit["mean"], c, "mean", 2))

        def square_sum(values, bias, total):
            squares = loads.tile([P, CHUNK], BF16, tag="squares", bufs=1)
            nc.scalar.activation(
                out=squares[:, 0 : values.shape[1]], in_=values, func=ACT.Square, bias=bias, accum_out=total
            )

        gate = const.tile([P, 1], F32)
        live_std = {}

        def phase1_std(unit, c):
            if not inside(c):
                return
            chunk = vpool.tile([P, CHUNK], F32, tag="v1")
            nc.scalar.activation(out=chunk[:], in_=unit["logvars"][c][:], func=ACT.Exp, scale=0.5)
            unit["chunks"].append(chunk)
            live_std[(unit["side"], c)] = chunk

        def phase1_first(unit, other, c):
            chunk = vpool.tile([P, CHUNK], F32, tag="v0")
            for part in halves if unit["side"] == FEATURES and c == 0 else (slice(0, CHUNK),):
                nc.vector.tensor_mul(
                    out=chunk[:, part], in0=unit["noises"][c][:, part], in1=other["chunks"][c][:, part]
                )
            unit["chunks"].append(chunk)

        def phase1_second_start(unit, c):
            chunk = unit["chunks"][c]
            live_std[(unit["side"], c)] = None
            early = slice(0, VECTOR_SHARE if c > 0 else CHUNK)
            nc.vector.tensor_mul(
                out=chunk[:, early], in0=unit["noises"][c][:, early], in1=chunk[:, early]
            )

        def phase1_second(unit, c):
            chunk = unit["chunks"][c]
            if quantised:
                gate_on_quantise()
            else:
                nc.gpsimd.tensor_copy(out=gate[:], in_=unit["v_sum"][:, c - 1 : c])
            late = slice(VECTOR_SHARE, CHUNK)
            nc.gpsimd.tensor_tensor(
                out=chunk[:, late], in0=unit["noises"][c][:, late], in1=chunk[:, late], op=ALU.mult
            )

        def phase1_sum(unit, c):
            v = unit["chunks"][c]
            nc.vector.scalar_tensor_tensor(
                out=v[:], in0=v[:], scalar=1.0, in1=unit["means"][c][:],
                op0=ALU.mult, op1=ALU.add, accum_out=unit["v_sum"][:, c : c + 1],
            )
            if c == 0:
                nc.vector.tensor_scalar_mul(
                    out=unit["neg_shift"][:], in0=unit["v_sum"][:, 0:1], scalar1=-1.0 / CHUNK
                )
            square_sum(v[:], unit["neg_shift"][:], unit["v_sq"][:, c : c + 1])

        def mean_statistics(kept):
            mu = stats.tile([P, 1], F32)
            nc.vector.reduce_sum(out=mu[:], in_=kept["v_sum"][:], axis=AXIS_X)
            nc.gpsimd.tensor_scalar(
                out=mu[:], in0=mu[:], scalar1=1.0 / K, scalar2=0.0, op0=ALU.mult, op1=ALU.add
            )
            off = stats.tile([P, 1], F32)
            nc.gpsimd.tensor_tensor(out=off[:], in0=mu[:], in1=kept["neg_shift"][:], op=ALU.add)
            nc.gpsimd.tensor_tensor(out=off[:], in0=off[:], in1=off[:], op=ALU.mult)
            nc.gpsimd.tensor_scalar(
                out=off[:], in0=off[:], scalar1=1.0, scalar2=-LN_EPS, op0=ALU.mult, op1=ALU.add
            )
            kept["mu"] = mu
            kept["off"] = off

        def variance_statistics(kept):
            var = stats.tile([P, 1], F32)
            nc.vector.reduce_sum(out=var[:], in_=kept["v_sq"][:], axis=AXIS_X)
            nc.vector.scalar_tensor_tensor(
                out=var[:], in0=var[:], scalar=1.0 / K, in1=kept["off"][:],
                op0=ALU.mult, op1=ALU.subtract,
            )
            rstd = stats.tile([P, 1], F32)
            nc.gpsimd.tensor_tensor(out=rstd[:], in0=var[:], in1=neg_half[:], op=ALU.pow)
            kept["rstd"] = rstd

        def phase2_spread(unit, c):
            unit["gain"] = []
            unit["bias"] = []
            for first in range(0, CHUNK, BANK_BF16):
                unit["gain"].append(spread_over_partitions((c * CHUNK + first) // (2 * P), "gain"))
            for first in range(0, CHUNK, BANK_BF16):
                unit["bias"].append(
                    spread_over_partitions(BIAS_COLUMN + (c * CHUNK + first) // (2 * P), "bias")
                )

        def phase2_apply(unit, c):
            v = unit["chunks"][c]
            for half in range(CHUNK // BANK_BF16):
                part = v[:, half * BANK_BF16 : (half + 1) * BANK_BF16]
                nc.vector.scalar_tensor_tensor(
                    out=part, in0=part, scalar=unit["mu"][:], in1=unit["gain"][half],
                    op0=ALU.subtract, op1=ALU.mult,
                )
            for half in range(CHUNK // BANK_BF16):
                part = v[:, half * BANK_BF16 : (half + 1) * BANK_BF16]
                nc.vector.scalar_tensor_tensor(
                    out=part, in0=part, scalar=unit["rstd"][:], in1=unit["bias"][half],
                    op0=ALU.mult, op1=ALU.add,
                )

        def phase2_square(unit, c):
            u = unit["chunks"][c]
            total = unit["u_sq"][:, c : c + 1]
            if unit["sample"] == 0 or c < N_CHUNKS - 1:
                square_sum(u[:], 0.0, total)
                return
            half = CHUNK // 2
            square_sum(u[:, 0:half], 0.0, total)
            unread = rows.tile([P, half], BF16, tag="row16", bufs=3)
            nc.vector.scalar_tensor_tensor(
                out=unread[:], in0=u[:, half:CHUNK], scalar=1.0, in1=u[:, half:CHUNK],
                op0=ALU.mult, op1=ALU.mult, accum_out=unit["u_sq"][:, N_CHUNKS : N_CHUNKS + 1],
            )

        def l2_norm_statistics(kept):
            norm2 = stats.tile([P, 1], F32)
            nc.vector.reduce_sum(out=norm2[:], in_=kept["u_sq"][:], axis=AXIS_X)
            nc.gpsimd.tensor_scalar(
                out=norm2[:], in0=norm2[:], scalar1=1e-24, scalar2=0.0, op0=ALU.max, op1=ALU.add
            )
            inv_norm = stats.tile([P, 1], F32)
            nc.gpsimd.tensor_tensor(out=inv_norm[:], in0=norm2[:], in1=neg_half[:], op=ALU.pow)
            kept["inv_norm"] = inv_norm

        def phase3_round(unit, c, engine):
            if not inside(c):
                return
            unit16 = rows.tile([P, CHUNK], BF16, tag="row16", bufs=3)
            if engine == nc.scalar:
                nc.scalar.activation(
                    out=unit16[:], in_=unit["chunks"][c][:], func=ACT.Copy, scale=unit["inv_norm"][:]
                )
            else:
                engine.tensor_scalar(
                    out=unit16[:], in0=unit["chunks"][c][:], scalar1=unit["inv_norm"][:],
                    scalar2=0.0, op0=ALU.mult, op1=ALU.add,
                )
            unit["rounded"].append(unit16)

        def phase3_turn(unit, c, copies):
            if inside(c):
                unit["grouped"].append(turn_rows(unit["rounded"][c], copies))

        def phase3_quantise(unit, c):
            if not inside(c):
                return
            sample = unit["sample"]
            grouped = unit["grouped"][c]
            if unit["side"] == FEATURES:
                chunk_words = slice(c * WORDS_PER_CHUNK, (c + 1) * WORDS_PER_CHUNK)
                quantise(grouped, x_codes[sample][:, chunk_words], x_scales[sample][:, chunk_words])
                return
            p_codes = packs.tile([P, WORDS_PER_CHUNK], U32, align_bytes=64, tag="codes", bufs=2)
            p_scales = packs.tile([P, WORDS_PER_CHUNK], U8, align_bytes=64, tag="scales", bufs=2)
            quantise(grouped, p_codes[:], p_scales[:])
            for g in range(PASSES_PER_CHUNK):
                one = slice(g * P, (g + 1) * P)
                x_one = slice(c * WORDS_PER_CHUNK + g * P, c * WORDS_PER_CHUNK + (g + 1) * P)
                for r in range(SAMPLES):
                    nc.tensor.matmul_mx(
                        out=sim_sum[:],
                        lhsT=x_codes[r][:, x_one].bitcast(FP8X4),
                        lhsT_scale=x_scales[r][:, x_one],
                        rhs=p_codes[:, one].bitcast(FP8X4),
                        rhs_scale=p_scales[:, one],
                        start=(sample == 0 and c == 0 and g == 0 and r == 0),
                        stop=(
                            sample == SAMPLES - 1
                            and c == N_CHUNKS - 1
                            and g == PASSES_PER_CHUNK - 1
                            and r == SAMPLES - 1
                        ),
                    )

        cross_done = []
        cross = {"count": 0, "loaded": [], "started": [], "turned": []}

        def cross_load():
            held_tiles = len(cross["loaded"]) + len(cross["started"])
            if cross["count"] < len(CROSS_ORDER) and held_tiles < 2:
                side, j = CROSS_ORDER[cross["count"]]
                cross["loaded"].append(load(units[2 * side]["logvar"], j, "cross_logvar", 2))
                cross["count"] = cross["count"] + 1

        def cross_piece():
            if cross["started"]:
                side, j, std16, made = cross["started"][0]
                if not made:
                    nc.scalar.activation(out=std16[:], in_=std16[:], func=ACT.Exp, scale=0.5)
                    cross["started"].clear()
                    cross["started"].append((side, j, std16, True))
                return
            if not cross["loaded"]:
                return
            side, j = CROSS_ORDER[cross["count"] - len(cross["loaded"])]
            logvar = cross["loaded"][0]
            cross["loaded"].remove(logvar)
            total = (xv_parts, pv_parts)[side][:, j : j + 1]
            std = live_std.get((side, j), None)
            if std is None:
                unread = loads.tile([P, CHUNK], BF16, tag="squares", bufs=1)
                nc.scalar.activation(out=unread[:], in_=logvar[:], func=ACT.Exp, accum_out=total)
                cross["started"].append((side, j, logvar, False))
            else:
                std16 = rows.tile([P, CHUNK], BF16, tag="row16", bufs=3)
                nc.vector.tensor_copy(out=std16[:], in_=std[:])
                nc.scalar.activation(out=logvar[:], in_=logvar[:], func=ACT.Exp, accum_out=total)
                cross["started"].append((side, j, std16, True))

        def cross_turn(copies, room):
            if cross["started"] and cross["started"][0][3]:
                if len(cross["turned"]) >= room:
                    cross_finish(True)
                side, j, std16, made = cross["started"][0]
                cross["started"].clear()
                cross["turned"].append({"half": (side, j), "grouped": turn_rows(std16, copies), "age": 0})

        def cross_finish(now=False):
            if not cross["turned"]:
                return
            if not now:
                for turned in cross["turned"]:
                    turned["age"] = turned["age"] + 1
                if cross["turned"][0]["age"] < 2:
                    return
            oldest = cross["turned"][0]
            cross["turned"].remove(oldest)
            side, j = oldest["half"]
            grouped = oldest["grouped"]
            if side == FEATURES:
                codes = packs.tile([P, WORDS_PER_CHUNK], U32, align_bytes=64, tag="cross_codes", bufs=1)
                scales = packs.tile([P, WORDS_PER_CHUNK], U8, align_bytes=64, tag="cross_scales", bufs=1)
                quantise(grouped, codes[:], scales[:])
                cross["x"] = (codes, scales)
                return
            codes = packs.tile([P, WORDS_PER_CHUNK], U32, align_bytes=64, tag="codes", bufs=2)
            scales = packs.tile([P, WORDS_PER_CHUNK], U8, align_bytes=64, tag="scales", bufs=2)
            quantise(grouped, codes[:], scales[:])
            xc, xs = cross["x"]
            for g in range(PASSES_PER_CHUNK):
                one = slice(g * P, (g + 1) * P)
                nc.tensor.matmul_mx(
                    out=cross_sum[:],
                    lhsT=xc[:, one].bitcast(FP8X4),
                    lhsT_scale=xs[:, one],
                    rhs=codes[:, one].bitcast(FP8X4),
                    rhs_scale=scales[:, one],
                    start=(len(cross_done) == 0 and g == 0),
                    stop=(len(cross_done) == N_CHUNKS - 1 and g == PASSES_PER_CHUNK - 1),
                )
            cross_done.append(j)

        units = []
        for side in (FEATURES, PROTOTYPES):
            for sample in range(SAMPLES):
                v_sum = stats.tile([P, N_CHUNKS], F32)
                v_sq = stats.tile([P, N_CHUNKS], F32)
                u_sq = stats.tile([P, N_CHUNKS + sample], F32)
                neg_shift = stats.tile([P, 1], F32)
                mean_rows, logvar_rows, noise_rows = sides[side]
                units.append(
                    {
                        "side": side, "sample": sample, "mean": mean_rows, "logvar": logvar_rows,
                        "noise": noise_rows[sample], "v_sum": v_sum, "v_sq": v_sq, "u_sq": u_sq,
                        "neg_shift": neg_shift, "logvars": [], "noises": [], "means": [], "chunks": [],
                        "rounded": [], "grouped": [],
                    }
                )
        def inside(c):
            return 0 <= c < N_CHUNKS

        both = (nc.scalar.copy, nc.scalar.copy)
        ctx.enter_context(tc.manual_schedule())

        def extra(stage, i):
            cross_turn(both, 2 if stage == 1 or (stage in (2, 5) and i < 5) else 1)
            for piece in range(PIECES[stage][i]):
                cross_piece()

        x0, x1, p0, p1 = units
        halves = (slice(0, CHUNK // 2), slice(CHUNK // 2, CHUNK))
        logvar = loads.tile([P, CHUNK], BF16, tag="logvar", bufs=2)
        noise = loads.tile([P, CHUNK], BF16, tag="noise", bufs=3)
        x1["logvars"].append(logvar)
        x0["noises"].append(noise)
        for half in halves:
            nc.sync.dma_start(out=logvar[:, half], in_=x_var[:, half])
            nc.sync.dma_start(out=noise[:, half], in_=eps_x[0][:, half])
        load_logvar(x1, 1)
        load_mean(x0, 0)
        load_noise(x0, 1)
        std = vpool.tile([P, CHUNK], F32, tag="v1")
        x1["chunks"].append(std)
        live_std[(FEATURES, 0)] = std
        for half in halves:
            nc.scalar.activation(out=std[:, half], in_=logvar[:, half], func=ACT.Exp, scale=0.5)
        load_logvar(x1, 2)
        load_logvar(x1, 3)
        phase1_std(x1, 1)
        for first, second, third, s in ((x0, x1, None, 1), (p0, p1, x1, 4)):
            for i in range(N_CHUNKS + 1):
                load_logvar(second, i + (4 if third is None else 3))
                load_noise(first, i + 2)
                cross_load()
                if third is not None:
                    phase3_round(third, i + 2, nc.vector)
                phase1_std(second, i + 2)
                if inside(i):
                    phase1_first(first, second, i)
                if inside(i - 1):
                    phase1_sum(first, i - 1)
                load_mean(first, i + 1)
                if third is not None:
                    phase3_quantise(third, i)
                    phase3_turn(third, i + 2, both)
                cross_finish()
                extra(s, i)
            if s == 1:
                load_gain_and_bias()
                turn_gain_and_bias()
            load_noise(second, 0)
            load_noise(second, 1)
            load_mean(second, 0)
            mean_statistics(first)
            phase1_second_start(second, 0)
            variance_statistics(first)
            phase2_spread(first, 0)

            for i in range(N_CHUNKS):
                load_noise(second, i + 2)
                load_mean(second, i + 1)
                if inside(i + 1):
                    phase1_second_start(second, i + 1)
                quantised.clear()
                phase1_sum(second, i)
                cross_load()
                if inside(i - 1):
                    phase2_square(first, i - 1)
                cross_finish()
                if inside(i + 1):
                    phase1_second(second, i + 1)
                else:
                    mean_statistics(second)
                phase2_apply(first, i)
                phase2_spread(*((first, i + 1) if inside(i + 1) else (second, 0)))
                extra(s + 1, i)
            phase2_square(first, N_CHUNKS - 1)
            variance_statistics(second)

            for i in range(N_CHUNKS):
                cross_load()
                phase2_apply(second, i)
                if inside(i + 1):
                    phase2_spread(second, i + 1)
                if i == 0:
                    l2_norm_statistics(first)
                phase3_turn(first, i - 1, both)
                phase3_quantise(first, i - 2)
                cross_finish()
                gate_on_quantise()
                phase3_round(first, i, nc.gpsimd)
                phase2_square(second, i)
                extra(s + 2, i)
            phase3_turn(first, N_CHUNKS - 1, both)
            phase3_quantise(first, N_CHUNKS - 2)
            cross_finish(True)
            if s == 1:
                load_logvar(p1, 0)
                load_logvar(p1, 1)
                load_noise(p0, 0)
                load_mean(p0, 0)
                load_noise(p0, 1)
            l2_norm_statistics(second)
            phase3_round(second, 0, nc.vector)
            phase3_round(second, 1, nc.vector)
            phase3_quantise(first, N_CHUNKS - 1)
            if s == 1:
                for c in range(2):
                    phase1_std(p1, c)
                    phase3_turn(x1, c, both)
                load_logvar(p1, 2)

        xv_term = const.tile([P, 1], F32)
        pv_sum = const.tile([P, 1], F32)
        pv_repeated = const.tile([P, P], F32)
        result = const.tile([P, P], F32)

        def all_but_the_samples():
            nc.vector.reduce_sum(out=xv_term[:], in_=xv_parts[:], axis=AXIS_X)
            nc.vector.tensor_scalar(
                out=xv_term[:], in0=xv_term[:], scalar1=-LAMDA, scalar2=-2.0, op0=ALU.mult, op1=ALU.add
            )
            nc.vector.reduce_sum(out=pv_sum[:], in_=pv_parts[:], axis=AXIS_X)
            nc.vector.tensor_scalar(
                out=pv_repeated[:], in0=ident[:], scalar1=0.0, scalar2=pv_sum[:],
                op0=ALU.mult, op1=ALU.add,
            )
            pv_bank = spread.tile([P, BANK_WORDS], F32, tag="gain")
            pv_along = pv_bank[:, 0:P]
            nc.tensor.transpose(pv_along, pv_repeated[:], ident[:])

            nc.vector.tensor_scalar(
                out=result[:], in0=cross_sum[:], scalar1=2.0 * LAMDA, scalar2=xv_term[:],
                op0=ALU.mult, op1=ALU.add,
            )
            nc.vector.scalar_tensor_tensor(
                out=result[:], in0=pv_along, scalar=-LAMDA, in1=result[:],
                op0=ALU.mult, op1=ALU.add,
            )

        for i in range(N_CHUNKS + 2):
            cross_load()
            phase3_turn(p1, i, both)
            phase3_round(p1, i + 2, nc.vector)
            phase3_quantise(p1, i - 1)
            if i in (1, 4):
                cross_finish(True)
            extra(7, i)
            if i == N_CHUNKS - 2:
                all_but_the_samples()

        nc.vector.scalar_tensor_tensor(
            out=result[:], in0=sim_sum[:], scalar=0.5, in1=result[:], op0=ALU.mult, op1=ALU.add
        )
        nc.sync.dma_start(out=out.rearrange("n c m -> n (c m)"), in_=result[:])
